import numpy as np
import ml_dtypes


def mxq(x, axis, fmt="e4m3"):
    dtype, down = {"e4m3": (ml_dtypes.float8_e4m3fn, 7), "e5m2": (ml_dtypes.float8_e5m2, 14)}[fmt]
    v = np.moveaxis(np.asarray(x, np.float32).astype(ml_dtypes.bfloat16).astype(np.float64), axis, -1)
    blocks = v.reshape(v.shape[:-1] + (-1, 32))
    amax = np.abs(blocks).max(-1, keepdims=True)
    byte = np.maximum(np.where(amax > 0, np.frexp(amax)[1] - 1 + 127, 0) - down, 1)
    scale = np.exp2(byte - 127.0)
    codes = (blocks / scale).astype(np.float32).astype(dtype).astype(np.float64)
    return np.moveaxis((codes * scale).reshape(v.shape), -1, axis)


WIDE = False


def mx_kscale(k):
    if not WIDE:
        return np.ones(k)
    levels = np.array([10, -10, 5, -5, 0])
    a = np.random.permutation(np.resize(levels, k // 512 * 4)).reshape(k // 512, 4)
    idx = np.arange(k)
    return np.exp2(a[idx // 512, idx % 128 // 32])


BF16 = ml_dtypes.bfloat16


def bf(x):
    return np.asarray(x, np.float32).astype(BF16)


def f64(x):
    return np.asarray(x).astype(np.float64)


B, T, U, D_ENC, D_PRED, D_JOINT, VOCAB = 4, 128, 32, 512, 512, 512, 128
LOGIT_CLAMP = 15.0


def setup_inputs():
    se, sp = mx_kscale(D_ENC), mx_kscale(D_PRED)
    t = mx_kscale(D_JOINT)
    g = t / t.max()
    return {"encoder_out": bf(np.random.standard_normal((B, T, D_ENC)) * se),
            "predictor_out": bf(np.random.standard_normal((B, U, D_PRED)) * sp),
            "W_enc": bf(np.random.standard_normal((D_ENC, D_JOINT)) * 0.7 / np.sqrt(D_ENC) / se[:, None] * g),
            "b_enc": bf(np.random.standard_normal(D_JOINT) * 0.2 * g),
            "W_pred": bf(np.random.standard_normal((D_PRED, D_JOINT)) * 0.7 / np.sqrt(D_PRED) / sp[:, None] * g),
            "b_pred": bf(np.random.standard_normal(D_JOINT) * 0.2 * g),
            "W_out": bf(np.random.standard_normal((D_JOINT, VOCAB)) * 8.0 / np.sqrt(D_JOINT) / g[:, None]),
            "b_out": bf(np.random.standard_normal(VOCAB) * 0.5)}


def reference(encoder_out, predictor_out, W_enc, b_enc, W_pred, b_pred, W_out, b_out):
    enc = (mxq(f64(encoder_out), 2, "e4m3") @ mxq(f64(W_enc), 0, "e4m3")) + f64(b_enc)
    pred = (mxq(f64(predictor_out), 2, "e4m3") @ mxq(f64(W_pred), 0, "e4m3")) + f64(b_pred)
    joint = np.tanh(enc[:, :, None, :] + pred[:, None, :, :])
    logits = (mxq(joint, 3, "e4m3") @ mxq(f64(W_out), 0, "e4m3")) + f64(b_out)
    return np.clip(logits, -LOGIT_CLAMP, LOGIT_CLAMP)

@@ -1,0 +1,224 @@
+from contextlib import ExitStack
+
+import concourse.mybir as mybir
+from concourse.masks import make_identity
+
+F32 = mybir.dt.float32
+BF16 = mybir.dt.bfloat16
+U32 = mybir.dt.uint32
+U8 = mybir.dt.uint8
+FP8X4 = mybir.dt.float8_e4m3fn_x4
+ACTF = mybir.ActivationFunctionType
+ALU = mybir.AluOpType
+
+P = 128
+B, T, U, D, V = 4, 128, 32, 512, 128
+NCH = 4
+UG = 4
+CLAMP = 15.0
+FLOPS = 2 * (B * T * D * D + B * U * D * D + B * T * U * D * V)
+
+
+def regroup(eng_copy, dst, src):
+    eng_copy(
+        out=dst.rearrange("p (c i) j -> p c j i", i=4),
+        in_=src.rearrange("p j (c i) -> p c j i", i=4),
+    )
+
+
+def tile_jointnetwork_t_kernel(
+    tc, encoder_out, predictor_out, W_enc, b_enc, W_pred, b_pred, W_out, b_out, out
+):
+    nc = tc.nc
+    with ExitStack() as ctx:
+        keep = ctx.enter_context(tc.tile_pool(name="keep", bufs=1))
+        work = ctx.enter_context(tc.tile_pool(name="work", bufs=3))
+        psum = ctx.enter_context(tc.psum_pool(name="psum", bufs=2))
+
+        warm = keep.tile([P, 1], F32)
+        nc.vector.memset(warm[:], 0.0)
+        nc.scalar.activation(out=warm[:], in_=warm[:], func=ACTF.Tanh)
+        ident = keep.tile([P, P], F32)
+        make_identity(nc, ident[:])
+        bz = keep.tile([P, P], BF16)
+        nc.vector.memset(bz[:], 0.0)
+
+        x_sb = keep.tile([P, B, D], BF16)
+        nc.sync.dma_start(out=x_sb[:, 0, :], in_=encoder_out[0])
+        y_sb = keep.tile([P, D], BF16)
+        nc.sync.dma_start(out=y_sb[:], in_=predictor_out.rearrange("b u d -> (b u) d"))
+        we_raw = keep.tile([P, 4, D], BF16)
+        nc.sync.dma_start(
+            out=we_raw[:].rearrange("p (h e) c -> p h (e c)", h=2),
+            in_=W_enc.rearrange("(h q e) c -> q h (e c)", h=2, e=2),
+        )
+        wp_raw = keep.tile([P, 4, D], BF16)
+        nc.sync.dma_start(
+            out=wp_raw[:].rearrange("p (h e) c -> p h (e c)", h=2),
+            in_=W_pred.rearrange("(h q e) c -> q h (e c)", h=2, e=2),
+        )
+        nc.sync.dma_start(out=bz[0:4, :], in_=b_enc.rearrange("(c p) -> c p", p=P))
+        nc.sync.dma_start(out=bz[4:8, :], in_=b_pred.rearrange("(c p) -> c p", p=P))
+        nc.sync.dma_start(out=bz[8:9, :], in_=b_out.rearrange("(o v) -> o v", o=1))
+        wo_raw = keep.tile([P, NCH, V], BF16)
+        nc.sync.dma_start(out=wo_raw[:], in_=W_out.rearrange("(c p) v -> p c v", p=P))
+        nc.sync.dma_start(
+            out=x_sb[:, 1:B, :], in_=encoder_out[1:B].rearrange("b t d -> t b d")
+        )
+
+        x_g = keep.tile([P, B * T * 4], BF16, align_bytes=64)
+        x_codes = keep.tile([P, B * T], U32, align_bytes=64)
+        x_scales = keep.tile([P, B * T], U8, align_bytes=64)
+        y_g = keep.tile([P, P * 4], BF16, align_bytes=64)
+        y_codes = keep.tile([P, P], U32, align_bytes=64)
+        y_scales = keep.tile([P, P], U8, align_bytes=64)
+        we_g = keep.tile([P, D, 4], BF16, align_bytes=64)
+        we_codes = keep.tile([P, D], U32, align_bytes=64)
+        we_scales = keep.tile([P, D], U8, align_bytes=64)
+        wp_g = keep.tile([P, D, 4], BF16, align_bytes=64)
+        wp_codes = keep.tile([P, D], U32, align_bytes=64)
+        wp_scales = keep.tile([P, D], U8, align_bytes=64)
+        wo_g = keep.tile([P, V, 4], BF16, align_bytes=64)
+        wo_codes = keep.tile([P, V], U32, align_bytes=64)
+        wo_scales = keep.tile([P, V], U8, align_bytes=64)
+        enc_t = keep.tile([P, B, NCH, T], F32)
+        pred_b = keep.tile([P, NCH, B * U], F32)
+
+        def transpose_rows(rows_bf16, g_slice, copy_fn):
+            words = rows_bf16.bitcast(F32)
+            tr = psum.tile([P, 2, P], F32, tag="tr")
+            for h in range(2):
+                nc.tensor.transpose(tr[:, h, :], words[:, h * P : (h + 1) * P], ident[:])
+            copy_fn(
+                out=g_slice.bitcast(F32).rearrange("p (r h) -> p r h", h=2),
+                in_=tr[:].rearrange("p h r -> p r h"),
+            )
+
+        def setup_x(b, copy_fn):
+            cols = slice(b * T, (b + 1) * T)
+            gcols = slice(b * T * 4, (b + 1) * T * 4)
+            transpose_rows(x_sb[:, b, :], x_g[:, gcols], copy_fn)
+            nc.vector.quantize_mx(
+                out=x_codes[:, cols].bitcast(FP8X4), scales=x_scales[:, cols], in_=x_g[:, gcols]
+            )
+
+        def enc_matmul(b, copy_fn):
+            cols = slice(b * T, (b + 1) * T)
+            e_ps = psum.tile([P, NCH, T], F32, tag="mm")
+            for c in range(NCH):
+                kc = slice(c * P, (c + 1) * P)
+                nc.tensor.matmul_mx(
+                    out=e_ps[:, c, :],
+                    lhsT=we_codes[:, kc].bitcast(FP8X4),
+                    lhsT_scale=we_scales[:, kc],
+                    rhs=x_codes[:, cols].bitcast(FP8X4),
+                    rhs_scale=x_scales[:, cols],
+                    start=True,
+                    stop=True,
+                )
+            copy_fn(out=enc_t[:, b, :, :], in_=e_ps[:])
+
+        setup_x(0, nc.vector.tensor_copy)
+        transpose_rows(y_sb[:], y_g[:], nc.scalar.copy)
+        regroup(nc.vector.tensor_copy, we_g[:], we_raw[:])
+        nc.vector.quantize_mx(out=y_codes[:].bitcast(FP8X4), scales=y_scales[:], in_=y_g[:])
+        regroup(nc.scalar.copy, wp_g[:], wp_raw[:])
+        nc.vector.quantize_mx(
+            out=we_codes[:].bitcast(FP8X4),
+            scales=we_scales[:],
+            in_=we_g[:].rearrange("p w j -> p (w j)"),
+        )
+        bf = keep.tile([P, P], F32)
+        nc.vector.tensor_copy(out=bf[:], in_=bz[:])
+        bt_ps = psum.tile([P, P], F32, tag="tr")
+        nc.tensor.transpose(bt_ps[:], bf[:], ident[:])
+        b_t = keep.tile([P, 8], F32)
+        nc.vector.tensor_copy(out=b_t[:], in_=bt_ps[:, 0:8])
+        b_sum = keep.tile([P, NCH], F32)
+        nc.vector.tensor_add(out=b_sum[:], in0=b_t[:, 0:4], in1=b_t[:, 4:8])
+        bo_ps = psum.tile([P, V], F32, tag="tr")
+        nc.tensor.matmul(
+            out=bo_ps[:], lhsT=ident[:, 8:9].to_broadcast([P, P]), rhs=bf[:], start=True, stop=True
+        )
+        bo4 = keep.tile([P, UG, V], F32)
+        nc.vector.tensor_copy(out=bo4[:], in_=bo_ps[:].unsqueeze(1).to_broadcast([P, UG, V]))
+
+        enc_matmul(0, nc.scalar.copy)
+        nc.vector.quantize_mx(
+            out=wp_codes[:].bitcast(FP8X4),
+            scales=wp_scales[:],
+            in_=wp_g[:].rearrange("p w j -> p (w j)"),
+        )
+        p_ps = psum.tile([P, NCH, B * U], F32, tag="mm")
+        for c in range(NCH):
+            kc = slice(c * P, (c + 1) * P)
+            nc.tensor.matmul_mx(
+                out=p_ps[:, c, :],
+                lhsT=wp_codes[:, kc].bitcast(FP8X4),
+                lhsT_scale=wp_scales[:, kc],
+                rhs=y_codes[:].bitcast(FP8X4),
+                rhs_scale=y_scales[:],
+                start=True,
+                stop=True,
+            )
+        nc.vector.tensor_tensor(
+            out=pred_b[:],
+            in0=p_ps[:],
+            in1=b_sum[:].unsqueeze(2).to_broadcast([P, NCH, B * U]),
+            op=ALU.add,
+        )
+        regroup(nc.vector.tensor_copy, wo_g[:], wo_raw[:])
+        nc.vector.quantize_mx(
+            out=wo_codes[:].bitcast(FP8X4),
+            scales=wo_scales[:],
+            in_=wo_g[:].rearrange("p w j -> p (w j)"),
+        )
+
+        W_UNIT = UG * T
+        for b in range(B):
+            out_b = out[b].rearrange("t u v -> t (u v)")
+            for g in range(U // UG):
+                planes = work.tile([P, NCH, W_UNIT], BF16, tag="planes", bufs=4)
+                for ul in range(UG):
+                    col = b * U + g * UG + ul
+                    for c in range(NCH):
+                        nc.scalar.activation(
+                            out=planes[:, c, ul * T : (ul + 1) * T],
+                            in_=enc_t[:, b, c, :],
+                            func=ACTF.Tanh,
+                            bias=pred_b[:, c, col : col + 1],
+                            scale=1.0,
+                        )
+                j_g = work.tile([P, W_UNIT, 4], BF16, tag="j_g", align_bytes=64)
+                regroup(nc.vector.tensor_copy, j_g[:], planes[:])
+                j_codes = work.tile([P, W_UNIT], U32, tag="j_codes", align_bytes=64)
+                j_scales = work.tile([P, W_UNIT], U8, tag="j_scales", align_bytes=64)
+                nc.vector.quantize_mx(
+                    out=j_codes[:].bitcast(FP8X4),
+                    scales=j_scales[:],
+                    in_=j_g[:].rearrange("p w j -> p (w j)"),
+                )
+                o_ps = psum.tile([P, UG, V], F32, tag="o", bufs=4)
+                for ul in range(UG):
+                    rows = slice(ul * T, (ul + 1) * T)
+                    nc.tensor.matmul_mx(
+                        out=o_ps[:, ul, :],
+                        lhsT=j_codes[:, rows].bitcast(FP8X4),
+                        lhsT_scale=j_scales[:, rows],
+                        rhs=wo_codes[:].bitcast(FP8X4),
+                        rhs_scale=wo_scales[:],
+                        start=True,
+                        stop=True,
+                    )
+                o_sb = work.tile([P, UG, V], F32, tag="o_sb", bufs=4)
+                nc.vector.tensor_tensor(out=o_sb[:], in0=o_ps[:], in1=bo4[:], op=ALU.add)
+                nc.vector.tensor_scalar(
+                    out=o_sb[:], in0=o_sb[:], scalar1=CLAMP, scalar2=-CLAMP, op0=ALU.min, op1=ALU.max
+                )
+                nc.sync.dma_start(
+                    out=out_b[:, g * UG * V : (g + 1) * UG * V],
+                    in_=o_sb[:].rearrange("p u v -> p (u v)"),
+                )
+                if g == 1 and b + 1 < B:
+                    setup_x(b + 1, nc.vector.tensor_copy)
+                    enc_matmul(b + 1, nc.vector.tensor_copy)

@@ -212,7 +212,7 @@ def tile_jointnetwork_t_kernel(
                     )
                 o_sb = work.tile([P, UG, V], F32, tag="o_sb", bufs=4)
                 nc.vector.tensor_tensor(out=o_sb[:], in0=o_ps[:], in1=bo4[:], op=ALU.add)
-                nc.vector.tensor_scalar(
+                nc.gpsimd.tensor_scalar(
                     out=o_sb[:], in0=o_sb[:], scalar1=CLAMP, scalar2=-CLAMP, op0=ALU.min, op1=ALU.max
                 )
                 nc.sync.dma_start(

@@ -17,10 +17,15 @@ NCH = 4
 UG = 4
 CLAMP = 15.0
 FLOPS = 2 * (B * T * D * D + B * U * D * D + B * T * U * D * V)
+PIN = True
+FIRST = 2
+TAIL = [2, 1, 1]
+SETUP_AT = (2, 3, 4)
+LAG = 1
 
 
-def regroup(eng_copy, dst, src):
-    eng_copy(
+def regroup(copy_fn, dst, src):
+    copy_fn(
         out=dst.rearrange("p (c i) j -> p c j i", i=4),
         in_=src.rearrange("p j (c i) -> p c j i", i=4),
     )
@@ -31,194 +36,263 @@ def tile_jointnetwork_t_kernel(
 ):
     nc = tc.nc
     with ExitStack() as ctx:
+        if PIN:
+            ctx.enter_context(tc.manual_schedule())
         keep = ctx.enter_context(tc.tile_pool(name="keep", bufs=1))
         work = ctx.enter_context(tc.tile_pool(name="work", bufs=3))
         psum = ctx.enter_context(tc.psum_pool(name="psum", bufs=2))
 
+        def quantise(codes, scales, grouped):
+            nc.vector.quantize_mx(out=codes.bitcast(FP8X4), scales=scales, in_=grouped)
+
+        def mx(out_ps, l_codes, l_scales, r_codes, r_scales):
+            nc.tensor.matmul_mx(
+                out=out_ps,
+                lhsT=l_codes.bitcast(FP8X4),
+                lhsT_scale=l_scales,
+                rhs=r_codes.bitcast(FP8X4),
+                rhs_scale=r_scales,
+                start=True,
+                stop=True,
+            )
+
         warm = keep.tile([P, 1], F32)
-        nc.vector.memset(warm[:], 0.0)
-        nc.scalar.activation(out=warm[:], in_=warm[:], func=ACTF.Tanh)
         ident = keep.tile([P, P], F32)
-        make_identity(nc, ident[:])
         bz = keep.tile([P, P], BF16)
-        nc.vector.memset(bz[:], 0.0)
-
-        x_sb = keep.tile([P, B, D], BF16)
-        nc.sync.dma_start(out=x_sb[:, 0, :], in_=encoder_out[0])
+        bf = keep.tile([P, P], F32)
+        b_t = keep.tile([P, 8], F32)
+        bo4 = keep.tile([P, UG, V], F32)
         y_sb = keep.tile([P, D], BF16)
-        nc.sync.dma_start(out=y_sb[:], in_=predictor_out.rearrange("b u d -> (b u) d"))
-        we_raw = keep.tile([P, 4, D], BF16)
-        nc.sync.dma_start(
-            out=we_raw[:].rearrange("p (h e) c -> p h (e c)", h=2),
-            in_=W_enc.rearrange("(h q e) c -> q h (e c)", h=2, e=2),
-        )
-        wp_raw = keep.tile([P, 4, D], BF16)
-        nc.sync.dma_start(
-            out=wp_raw[:].rearrange("p (h e) c -> p h (e c)", h=2),
-            in_=W_pred.rearrange("(h q e) c -> q h (e c)", h=2, e=2),
-        )
-        nc.sync.dma_start(out=bz[0:4, :], in_=b_enc.rearrange("(c p) -> c p", p=P))
-        nc.sync.dma_start(out=bz[4:8, :], in_=b_pred.rearrange("(c p) -> c p", p=P))
-        nc.sync.dma_start(out=bz[8:9, :], in_=b_out.rearrange("(o v) -> o v", o=1))
+        x_sb = keep.tile([P, B, D], BF16)
+        we_raw = [keep.tile([P, 4, D // 2], BF16, name="we_raw%d" % h) for h in range(2)]
+        wp_raw = [keep.tile([P, 4, D // 2], BF16, name="wp_raw%d" % h) for h in range(2)]
         wo_raw = keep.tile([P, NCH, V], BF16)
-        nc.sync.dma_start(out=wo_raw[:], in_=W_out.rearrange("(c p) v -> p c v", p=P))
-        nc.sync.dma_start(
-            out=x_sb[:, 1:B, :], in_=encoder_out[1:B].rearrange("b t d -> t b d")
-        )
-
-        x_g = keep.tile([P, B * T * 4], BF16, align_bytes=64)
-        x_codes = keep.tile([P, B * T], U32, align_bytes=64)
-        x_scales = keep.tile([P, B * T], U8, align_bytes=64)
-        y_g = keep.tile([P, P * 4], BF16, align_bytes=64)
-        y_codes = keep.tile([P, P], U32, align_bytes=64)
-        y_scales = keep.tile([P, P], U8, align_bytes=64)
-        we_g = keep.tile([P, D, 4], BF16, align_bytes=64)
-        we_codes = keep.tile([P, D], U32, align_bytes=64)
-        we_scales = keep.tile([P, D], U8, align_bytes=64)
-        wp_g = keep.tile([P, D, 4], BF16, align_bytes=64)
-        wp_codes = keep.tile([P, D], U32, align_bytes=64)
-        wp_scales = keep.tile([P, D], U8, align_bytes=64)
+        xy_g = keep.tile([P, 2 * P * 4], BF16, align_bytes=64)
+        xy_codes = keep.tile([P, 2 * P], U32, align_bytes=64)
+        xy_scales = keep.tile([P, 2 * P], U8, align_bytes=64)
+        x_g = keep.tile([P, (B - 1) * T * 4], BF16, align_bytes=64)
+        x_codes = keep.tile([P, (B - 1) * T], U32, align_bytes=64)
+        x_scales = keep.tile([P, (B - 1) * T], U8, align_bytes=64)
+        w_g = keep.tile([P, NCH, 2 * P, 4], BF16, align_bytes=64)
+        w_codes = keep.tile([P, NCH, 2 * P], U32, align_bytes=64)
+        w_scales = keep.tile([P, NCH, 2 * P], U8, align_bytes=64)
         wo_g = keep.tile([P, V, 4], BF16, align_bytes=64)
         wo_codes = keep.tile([P, V], U32, align_bytes=64)
         wo_scales = keep.tile([P, V], U8, align_bytes=64)
         enc_t = keep.tile([P, B, NCH, T], F32)
         pred_b = keep.tile([P, NCH, B * U], F32)
 
+        nc.vector.memset(warm[:], 0.0)
+        nc.vector.memset(bz[:], 0.0)
+        make_identity(nc, ident[:])
+        nc.scalar.dma_start(out=bz[0:4, :], in_=b_enc.rearrange("(c p) -> c p", p=P))
+        nc.scalar.dma_start(out=bz[4:8, :], in_=b_pred.rearrange("(c p) -> c p", p=P))
+        nc.scalar.dma_start(out=bz[8:9, :], in_=b_out.rearrange("(o v) -> o v", o=1))
+        nc.scalar.activation(out=warm[:], in_=warm[:], func=ACTF.Tanh)
+        nc.sync.dma_start(out=y_sb[:], in_=predictor_out.rearrange("b u d -> (b u) d"))
+        nc.sync.dma_start(out=x_sb[:, 0, :], in_=encoder_out[0])
+        for h in range(2):
+            cols = slice(h * (D // 2), (h + 1) * (D // 2))
+            nc.sync.dma_start(out=we_raw[h][:], in_=W_enc[:, cols].rearrange("(p j) c -> p j c", j=4))
+            nc.sync.dma_start(out=wp_raw[h][:], in_=W_pred[:, cols].rearrange("(p j) c -> p j c", j=4))
+        nc.sync.dma_start(out=wo_raw[:], in_=W_out.rearrange("(c p) v -> p c v", p=P))
+        nc.sync.dma_start(out=x_sb[:, 1:B, :], in_=encoder_out[1:B].rearrange("b t d -> t b d"))
+
         def transpose_rows(rows_bf16, g_slice, copy_fn):
-            words = rows_bf16.bitcast(F32)
+            words = rows_bf16.bitcast(F32).rearrange("r (q h) -> r h q", h=2)
             tr = psum.tile([P, 2, P], F32, tag="tr")
             for h in range(2):
-                nc.tensor.transpose(tr[:, h, :], words[:, h * P : (h + 1) * P], ident[:])
+                nc.tensor.transpose(tr[:, h, :], words[:, h, :], ident[:])
             copy_fn(
                 out=g_slice.bitcast(F32).rearrange("p (r h) -> p r h", h=2),
                 in_=tr[:].rearrange("p h r -> p r h"),
             )
 
-        def setup_x(b, copy_fn):
-            cols = slice(b * T, (b + 1) * T)
-            gcols = slice(b * T * 4, (b + 1) * T * 4)
-            transpose_rows(x_sb[:, b, :], x_g[:, gcols], copy_fn)
-            nc.vector.quantize_mx(
-                out=x_codes[:, cols].bitcast(FP8X4), scales=x_scales[:, cols], in_=x_g[:, gcols]
-            )
-
-        def enc_matmul(b, copy_fn):
-            cols = slice(b * T, (b + 1) * T)
-            e_ps = psum.tile([P, NCH, T], F32, tag="mm")
-            for c in range(NCH):
-                kc = slice(c * P, (c + 1) * P)
-                nc.tensor.matmul_mx(
-                    out=e_ps[:, c, :],
-                    lhsT=we_codes[:, kc].bitcast(FP8X4),
-                    lhsT_scale=we_scales[:, kc],
-                    rhs=x_codes[:, cols].bitcast(FP8X4),
-                    rhs_scale=x_scales[:, cols],
-                    start=True,
-                    stop=True,
-                )
-            copy_fn(out=enc_t[:, b, :, :], in_=e_ps[:])
-
-        setup_x(0, nc.vector.tensor_copy)
-        transpose_rows(y_sb[:], y_g[:], nc.scalar.copy)
-        regroup(nc.vector.tensor_copy, we_g[:], we_raw[:])
-        nc.vector.quantize_mx(out=y_codes[:].bitcast(FP8X4), scales=y_scales[:], in_=y_g[:])
-        regroup(nc.scalar.copy, wp_g[:], wp_raw[:])
-        nc.vector.quantize_mx(
-            out=we_codes[:].bitcast(FP8X4),
-            scales=we_scales[:],
-            in_=we_g[:].rearrange("p w j -> p (w j)"),
-        )
-        bf = keep.tile([P, P], F32)
+        transpose_rows(y_sb[:], xy_g[:, 0 : P * 4], nc.scalar.copy)
+        transpose_rows(x_sb[:, 0, :], xy_g[:, P * 4 : 2 * P * 4], nc.scalar.copy)
         nc.vector.tensor_copy(out=bf[:], in_=bz[:])
         bt_ps = psum.tile([P, P], F32, tag="tr")
         nc.tensor.transpose(bt_ps[:], bf[:], ident[:])
-        b_t = keep.tile([P, 8], F32)
-        nc.vector.tensor_copy(out=b_t[:], in_=bt_ps[:, 0:8])
-        b_sum = keep.tile([P, NCH], F32)
-        nc.vector.tensor_add(out=b_sum[:], in0=b_t[:, 0:4], in1=b_t[:, 4:8])
         bo_ps = psum.tile([P, V], F32, tag="tr")
         nc.tensor.matmul(
             out=bo_ps[:], lhsT=ident[:, 8:9].to_broadcast([P, P]), rhs=bf[:], start=True, stop=True
         )
-        bo4 = keep.tile([P, UG, V], F32)
+
+        def r_w(raw, c, side):
+            cc = (c % 2) * P
+            regroup(
+                nc.vector.tensor_copy,
+                w_g[:, c, side * P : (side + 1) * P, :],
+                raw[c // 2][:, :, cc : cc + P],
+            )
+
+        def q_w(c):
+            quantise(w_codes[:, c, :], w_scales[:, c, :], w_g[:, c, :, :].rearrange("p w j -> p (w j)"))
+
+        e0_ps = [None] * NCH
+        p_ps = [None] * NCH
+
+        def mm_chunk(c):
+            e0_ps[c] = psum.tile([P, T], F32, tag="o%d" % c, bufs=1, name="e0_ps_%d" % c)
+            mx(e0_ps[c][:], w_codes[:, c, 0:P], w_scales[:, c, 0:P], xy_codes[:, P : 2 * P], xy_scales[:, P : 2 * P])
+            p_ps[c] = psum.tile([P, B * U], F32, tag="mm", name="p_ps%d" % c)
+            mx(p_ps[c][:], w_codes[:, c, P : 2 * P], w_scales[:, c, P : 2 * P], xy_codes[:, 0:P], xy_scales[:, 0:P])
+
+        def predb(c):
+            nc.vector.tensor_scalar(
+                out=pred_b[:, c, :],
+                in0=p_ps[c][:],
+                scalar1=b_t[:, c : c + 1],
+                scalar2=b_t[:, NCH + c : NCH + c + 1],
+                op0=ALU.add,
+                op1=ALU.add,
+            )
+
+        r_w(we_raw, 0, 0)
+        r_w(we_raw, 1, 0)
+        quantise(xy_codes[:], xy_scales[:], xy_g[:])
+        nc.vector.tensor_copy(out=b_t[:], in_=bt_ps[:, 0:8])
+        r_w(wp_raw, 0, 1)
+        r_w(wp_raw, 1, 1)
+        q_w(0)
+        mm_chunk(0)
+        q_w(1)
+        mm_chunk(1)
+        r_w(we_raw, 2, 0)
+        predb(0)
+        r_w(we_raw, 3, 0)
+        predb(1)
+        r_w(wp_raw, 2, 1)
+        r_w(wp_raw, 3, 1)
+        q_w(2)
+        mm_chunk(2)
+        q_w(3)
+        mm_chunk(3)
+        regroup(nc.vector.tensor_copy, wo_g[:], wo_raw[:])
+        predb(2)
+        predb(3)
+        quantise(wo_codes[:], wo_scales[:], wo_g[:].rearrange("p w j -> p (w j)"))
         nc.vector.tensor_copy(out=bo4[:], in_=bo_ps[:].unsqueeze(1).to_broadcast([P, UG, V]))
 
-        enc_matmul(0, nc.scalar.copy)
-        nc.vector.quantize_mx(
-            out=wp_codes[:].bitcast(FP8X4),
-            scales=wp_scales[:],
-            in_=wp_g[:].rearrange("p w j -> p (w j)"),
-        )
-        p_ps = psum.tile([P, NCH, B * U], F32, tag="mm")
-        for c in range(NCH):
-            kc = slice(c * P, (c + 1) * P)
-            nc.tensor.matmul_mx(
-                out=p_ps[:, c, :],
-                lhsT=wp_codes[:, kc].bitcast(FP8X4),
-                lhsT_scale=wp_scales[:, kc],
-                rhs=y_codes[:].bitcast(FP8X4),
-                rhs_scale=y_scales[:],
-                start=True,
-                stop=True,
-            )
-        nc.vector.tensor_tensor(
-            out=pred_b[:],
-            in0=p_ps[:],
-            in1=b_sum[:].unsqueeze(2).to_broadcast([P, NCH, B * U]),
-            op=ALU.add,
-        )
-        regroup(nc.vector.tensor_copy, wo_g[:], wo_raw[:])
-        nc.vector.quantize_mx(
-            out=wo_codes[:].bitcast(FP8X4),
-            scales=wo_scales[:],
-            in_=wo_g[:].rearrange("p w j -> p (w j)"),
-        )
-
-        W_UNIT = UG * T
+        units = []
         for b in range(B):
-            out_b = out[b].rearrange("t u v -> t (u v)")
-            for g in range(U // UG):
-                planes = work.tile([P, NCH, W_UNIT], BF16, tag="planes", bufs=4)
-                for ul in range(UG):
-                    col = b * U + g * UG + ul
-                    for c in range(NCH):
-                        nc.scalar.activation(
-                            out=planes[:, c, ul * T : (ul + 1) * T],
-                            in_=enc_t[:, b, c, :],
-                            func=ACTF.Tanh,
-                            bias=pred_b[:, c, col : col + 1],
-                            scale=1.0,
-                        )
-                j_g = work.tile([P, W_UNIT, 4], BF16, tag="j_g", align_bytes=64)
-                regroup(nc.vector.tensor_copy, j_g[:], planes[:])
-                j_codes = work.tile([P, W_UNIT], U32, tag="j_codes", align_bytes=64)
-                j_scales = work.tile([P, W_UNIT], U8, tag="j_scales", align_bytes=64)
-                nc.vector.quantize_mx(
-                    out=j_codes[:].bitcast(FP8X4),
-                    scales=j_scales[:],
-                    in_=j_g[:].rearrange("p w j -> p (w j)"),
-                )
-                o_ps = psum.tile([P, UG, V], F32, tag="o", bufs=4)
-                for ul in range(UG):
-                    rows = slice(ul * T, (ul + 1) * T)
-                    nc.tensor.matmul_mx(
-                        out=o_ps[:, ul, :],
-                        lhsT=j_codes[:, rows].bitcast(FP8X4),
-                        lhsT_scale=j_scales[:, rows],
-                        rhs=wo_codes[:].bitcast(FP8X4),
-                        rhs_scale=wo_scales[:],
-                        start=True,
-                        stop=True,
-                    )
-                o_sb = work.tile([P, UG, V], F32, tag="o_sb", bufs=4)
-                nc.vector.tensor_tensor(out=o_sb[:], in0=o_ps[:], in1=bo4[:], op=ALU.add)
-                nc.gpsimd.tensor_scalar(
-                    out=o_sb[:], in0=o_sb[:], scalar1=CLAMP, scalar2=-CLAMP, op0=ALU.min, op1=ALU.max
-                )
-                nc.sync.dma_start(
-                    out=out_b[:, g * UG * V : (g + 1) * UG * V],
-                    in_=o_sb[:].rearrange("p u v -> p (u v)"),
-                )
-                if g == 1 and b + 1 < B:
-                    setup_x(b + 1, nc.vector.tensor_copy)
-                    enc_matmul(b + 1, nc.vector.tensor_copy)
+            sizes = [UG] * (U // UG)
+            if b == B - 1:
+                sizes = sizes[: -1] + TAIL
+            u0 = 0
+            for n in sizes:
+                units.append((b, u0, n))
+                u0 += n
+            assert u0 == U
+
+        planes = {}
+        j_codes = {}
+        j_scales = {}
+        j_g = {}
+        o_ps = {}
+
+        def new_planes(i):
+            planes[i] = work.tile([P, NCH, UG * T], BF16, tag="planes%d" % (i % 4), bufs=1, name="planes_%d" % i)
+
+        def tanh(i, c, ul):
+            b, u0, n = units[i]
+            col = b * U + u0 + ul
+            nc.scalar.activation(
+                out=planes[i][:, c, ul * T : (ul + 1) * T],
+                in_=enc_t[:, b, c, :],
+                func=ACTF.Tanh,
+                bias=pred_b[:, c, col : col + 1],
+                scale=1.0,
+            )
+
+        def r_j(i):
+            n = units[i][2]
+            j_g[i] = work.tile([P, UG * T, 4], BF16, tag="j_g%d" % (i % 3), bufs=1, align_bytes=64, name="j_g_%d" % i)
+            regroup(nc.vector.tensor_copy, j_g[i][:, 0 : n * T, :], planes[i][:, :, 0 : n * T])
+
+        def q_j(i):
+            n = units[i][2]
+            j_codes[i] = work.tile([P, UG * T], U32, tag="j_codes%d" % (i % 3), bufs=1, align_bytes=64, name="j_codes_%d" % i)
+            j_scales[i] = work.tile([P, UG * T], U8, tag="j_scales%d" % (i % 3), bufs=1, align_bytes=64, name="j_scales_%d" % i)
+            quantise(
+                j_codes[i][:, 0 : n * T],
+                j_scales[i][:, 0 : n * T],
+                j_g[i][:, 0 : n * T, :].rearrange("p w j -> p (w j)"),
+            )
+
+        def mm_j(i):
+            n = units[i][2]
+            o_ps[i] = psum.tile([P, UG, V], F32, tag="o%d" % (i % 4), bufs=1, name="o_ps_%d" % i)
+            for ul in range(n):
+                rows = slice(ul * T, (ul + 1) * T)
+                mx(o_ps[i][:, ul, :], j_codes[i][:, rows], j_scales[i][:, rows], wo_codes[:], wo_scales[:])
+
+        o_sbs = {}
+
+        def evac(i):
+            b, u0, n = units[i]
+            o_sb = work.tile([P, UG, V], F32, tag="o_sb%d" % (i % 6), bufs=1, name="o_sb_%d" % i)
+            nc.vector.tensor_tensor(out=o_sb[:, 0:n, :], in0=o_ps[i][:, 0:n, :], in1=bo4[:, 0:n, :], op=ALU.add)
+            o_sbs[i] = o_sb
+
+        def clamp_store(i):
+            b, u0, n = units[i]
+            o_sb = o_sbs[i]
+            nc.vector.tensor_scalar(
+                out=o_sb[:, 0:n, :], in0=o_sb[:, 0:n, :], scalar1=CLAMP, scalar2=-CLAMP, op0=ALU.min, op1=ALU.max
+            )
+            nc.sync.dma_start(
+                out=out[b].rearrange("t u v -> t (u v)")[:, u0 * V : (u0 + n) * V],
+                in_=o_sb[:, 0:n, :].rearrange("p u v -> p (u v)"),
+            )
+
+        def setup_x(b, step):
+            k = b - 1
+            cols = slice(k * T, (k + 1) * T)
+            gcols = slice(k * T * 4, (k + 1) * T * 4)
+            if step == 0:
+                transpose_rows(x_sb[:, b, :], x_g[:, gcols], nc.vector.tensor_copy)
+            elif step == 1:
+                quantise(x_codes[:, cols], x_scales[:, cols], x_g[:, gcols])
+                e_ps = psum.tile([P, NCH, T], F32, tag="mm", name="e_ps%d" % b)
+                for c in range(NCH):
+                    mx(e_ps[:, c, :], w_codes[:, c, 0:P], w_scales[:, c, 0:P], x_codes[:, cols], x_scales[:, cols])
+                o_ps["e%d" % b] = e_ps
+            else:
+                nc.vector.tensor_copy(out=enc_t[:, b, :, :], in_=o_ps["e%d" % b][:])
+
+        for i in range(FIRST):
+            new_planes(i)
+        for c in range(NCH):
+            nc.scalar.copy(out=enc_t[:, 0, c, :], in_=e0_ps[c][:])
+            for i in range(FIRST):
+                for ul in range(units[i][2]):
+                    tanh(i, c, ul)
+        for i in range(FIRST):
+            r_j(i)
+        for i in range(FIRST):
+            q_j(i)
+            mm_j(i)
+        done = 0
+        for i in range(FIRST, len(units)):
+            b, u0, n = units[i]
+            new_planes(i)
+            for ul in range(n):
+                for c in range(NCH):
+                    tanh(i, c, ul)
+            r_j(i)
+            first_new = done
+            while done < i - LAG:
+                evac(done)
+                done += 1
+            q_j(i)
+            mm_j(i)
+            for k in range(first_new, done):
+                clamp_store(k)
+            g = u0 // UG
+            if b + 1 < B and g in SETUP_AT and u0 % UG == 0:
+                setup_x(b + 1, SETUP_AT.index(g))
+        while done < len(units):
+            evac(done)
+            clamp_store(done)
+            done += 1

@@ -14,14 +14,14 @@ ALU = mybir.AluOpType
 P = 128
 B, T, U, D, V = 4, 128, 32, 512, 128
 NCH = 4
-UG = 4
+UB = 4
+UMAX = 4
 CLAMP = 15.0
 FLOPS = 2 * (B * T * D * D + B * U * D * D + B * T * U * D * V)
-PIN = True
+PIN = False
 FIRST = 2
-TAIL = [2, 1, 1]
-SETUP_AT = (2, 3, 4)
 LAG = 1
+SETUP_U = (8, 12, 16)
 
 
 def regroup(copy_fn, dst, src):
@@ -39,7 +39,7 @@ def tile_jointnetwork_t_kernel(
         if PIN:
             ctx.enter_context(tc.manual_schedule())
         keep = ctx.enter_context(tc.tile_pool(name="keep", bufs=1))
-        work = ctx.enter_context(tc.tile_pool(name="work", bufs=3))
+        work = ctx.enter_context(tc.tile_pool(name="work", bufs=1))
         psum = ctx.enter_context(tc.psum_pool(name="psum", bufs=2))
 
         def quantise(codes, scales, grouped):
@@ -61,7 +61,7 @@ def tile_jointnetwork_t_kernel(
         bz = keep.tile([P, P], BF16)
         bf = keep.tile([P, P], F32)
         b_t = keep.tile([P, 8], F32)
-        bo4 = keep.tile([P, UG, V], F32)
+        bo4 = keep.tile([P, UB, V], F32)
         y_sb = keep.tile([P, D], BF16)
         x_sb = keep.tile([P, B, D], BF16)
         we_raw = [keep.tile([P, 4, D // 2], BF16, name="we_raw%d" % h) for h in range(2)]
@@ -172,13 +172,15 @@ def tile_jointnetwork_t_kernel(
         predb(2)
         predb(3)
         quantise(wo_codes[:], wo_scales[:], wo_g[:].rearrange("p w j -> p (w j)"))
-        nc.vector.tensor_copy(out=bo4[:], in_=bo_ps[:].unsqueeze(1).to_broadcast([P, UG, V]))
+        nc.vector.tensor_copy(out=bo4[:], in_=bo_ps[:].unsqueeze(1).to_broadcast([P, UB, V]))
 
         units = []
         for b in range(B):
-            sizes = [UG] * (U // UG)
+            sizes = [4] * 8
+            if b == 0:
+                sizes = [4] * 8
             if b == B - 1:
-                sizes = sizes[: -1] + TAIL
+                sizes = [4] * 7 + [2, 1, 1]
             u0 = 0
             for n in sizes:
                 units.append((b, u0, n))
@@ -190,9 +192,12 @@ def tile_jointnetwork_t_kernel(
         j_scales = {}
         j_g = {}
         o_ps = {}
+        o_sbs = {}
+        e_pss = {}
+        bank_no = [0]
 
         def new_planes(i):
-            planes[i] = work.tile([P, NCH, UG * T], BF16, tag="planes%d" % (i % 4), bufs=1, name="planes_%d" % i)
+            planes[i] = work.tile([P, NCH, UMAX * T], BF16, tag="planes%d" % (i % 4), name="planes_%d" % i)
 
         def tanh(i, c, ul):
             b, u0, n = units[i]
@@ -207,13 +212,13 @@ def tile_jointnetwork_t_kernel(
 
         def r_j(i):
             n = units[i][2]
-            j_g[i] = work.tile([P, UG * T, 4], BF16, tag="j_g%d" % (i % 3), bufs=1, align_bytes=64, name="j_g_%d" % i)
+            j_g[i] = work.tile([P, UMAX * T, 4], BF16, tag="j_g%d" % (i % 3), align_bytes=64, name="j_g_%d" % i)
             regroup(nc.vector.tensor_copy, j_g[i][:, 0 : n * T, :], planes[i][:, :, 0 : n * T])
 
         def q_j(i):
             n = units[i][2]
-            j_codes[i] = work.tile([P, UG * T], U32, tag="j_codes%d" % (i % 3), bufs=1, align_bytes=64, name="j_codes_%d" % i)
-            j_scales[i] = work.tile([P, UG * T], U8, tag="j_scales%d" % (i % 3), bufs=1, align_bytes=64, name="j_scales_%d" % i)
+            j_codes[i] = work.tile([P, UMAX * T], U32, tag="j_codes%d" % (i % 3), align_bytes=64, name="j_codes_%d" % i)
+            j_scales[i] = work.tile([P, UMAX * T], U8, tag="j_scales%d" % (i % 3), align_bytes=64, name="j_scales_%d" % i)
             quantise(
                 j_codes[i][:, 0 : n * T],
                 j_scales[i][:, 0 : n * T],
@@ -222,18 +227,23 @@ def tile_jointnetwork_t_kernel(
 
         def mm_j(i):
             n = units[i][2]
-            o_ps[i] = psum.tile([P, UG, V], F32, tag="o%d" % (i % 4), bufs=1, name="o_ps_%d" % i)
-            for ul in range(n):
-                rows = slice(ul * T, (ul + 1) * T)
-                mx(o_ps[i][:, ul, :], j_codes[i][:, rows], j_scales[i][:, rows], wo_codes[:], wo_scales[:])
-
-        o_sbs = {}
+            o_ps[i] = []
+            for k0 in range(0, n, UB):
+                bank = psum.tile([P, UB, V], F32, tag="o%d" % (bank_no[0] % 4), bufs=1, name="o_ps_%d_%d" % (i, k0))
+                bank_no[0] += 1
+                o_ps[i].append(bank)
+                for ul in range(k0, min(n, k0 + UB)):
+                    rows = slice(ul * T, (ul + 1) * T)
+                    mx(bank[:, ul - k0, :], j_codes[i][:, rows], j_scales[i][:, rows], wo_codes[:], wo_scales[:])
 
         def evac(i):
-            b, u0, n = units[i]
-            o_sb = work.tile([P, UG, V], F32, tag="o_sb%d" % (i % 6), bufs=1, name="o_sb_%d" % i)
-            nc.vector.tensor_tensor(out=o_sb[:, 0:n, :], in0=o_ps[i][:, 0:n, :], in1=bo4[:, 0:n, :], op=ALU.add)
-            o_sbs[i] = o_sb
+            n = units[i][2]
+            o_sbs[i] = work.tile([P, UMAX, V], F32, tag="o_sb%d" % (i % 6), name="o_sb_%d" % i)
+            for k, bank in enumerate(o_ps[i]):
+                m = min(UB, n - k * UB)
+                nc.vector.tensor_tensor(
+                    out=o_sbs[i][:, k * UB : k * UB + m, :], in0=bank[:, 0:m, :], in1=bo4[:, 0:m, :], op=ALU.add
+                )
 
         def clamp_store(i):
             b, u0, n = units[i]
@@ -257,9 +267,9 @@ def tile_jointnetwork_t_kernel(
                 e_ps = psum.tile([P, NCH, T], F32, tag="mm", name="e_ps%d" % b)
                 for c in range(NCH):
                     mx(e_ps[:, c, :], w_codes[:, c, 0:P], w_scales[:, c, 0:P], x_codes[:, cols], x_scales[:, cols])
-                o_ps["e%d" % b] = e_ps
+                e_pss[b] = e_ps
             else:
-                nc.vector.tensor_copy(out=enc_t[:, b, :, :], in_=o_ps["e%d" % b][:])
+                nc.scalar.copy(out=enc_t[:, b, :, :], in_=e_pss[b][:])
 
         for i in range(FIRST):
             new_planes(i)
@@ -289,9 +299,8 @@ def tile_jointnetwork_t_kernel(
             mm_j(i)
             for k in range(first_new, done):
                 clamp_store(k)
-            g = u0 // UG
-            if b + 1 < B and g in SETUP_AT and u0 % UG == 0:
-                setup_x(b + 1, SETUP_AT.index(g))
+            if b + 1 < B and u0 in SETUP_U:
+                setup_x(b + 1, SETUP_U.index(u0))
         while done < len(units):
             evac(done)
             clamp_store(done)

@@ -15,11 +15,12 @@ P = 128
 B, T, U, D, V = 4, 128, 32, 512, 128
 NCH = 4
 UB = 4
-UMAX = 4
+UMAX = 8
 CLAMP = 15.0
 FLOPS = 2 * (B * T * D * D + B * U * D * D + B * T * U * D * V)
 PIN = False
-FIRST = 2
+FIRSTG = 2
+ACT_R = ((10, 0), (21, 0))
 LAG = 1
 SETUP_U = (8, 12, 16)
 
@@ -61,7 +62,7 @@ def tile_jointnetwork_t_kernel(
         bz = keep.tile([P, P], BF16)
         bf = keep.tile([P, P], F32)
         b_t = keep.tile([P, 8], F32)
-        bo4 = keep.tile([P, UB, V], F32)
+        bo = keep.tile([P, V], F32)
         y_sb = keep.tile([P, D], BF16)
         x_sb = keep.tile([P, B, D], BF16)
         we_raw = [keep.tile([P, 4, D // 2], BF16, name="we_raw%d" % h) for h in range(2)]
@@ -121,7 +122,7 @@ def tile_jointnetwork_t_kernel(
         def r_w(raw, c, side):
             cc = (c % 2) * P
             regroup(
-                nc.vector.tensor_copy,
+                nc.scalar.copy if side == 0 else nc.vector.tensor_copy,
                 w_g[:, c, side * P : (side + 1) * P, :],
                 raw[c // 2][:, :, cc : cc + P],
             )
@@ -172,19 +173,19 @@ def tile_jointnetwork_t_kernel(
         predb(2)
         predb(3)
         quantise(wo_codes[:], wo_scales[:], wo_g[:].rearrange("p w j -> p (w j)"))
-        nc.vector.tensor_copy(out=bo4[:], in_=bo_ps[:].unsqueeze(1).to_broadcast([P, UB, V]))
+        nc.vector.tensor_copy(out=bo[:], in_=bo_ps[:])
 
-        units = []
+        groups = []
         for b in range(B):
-            sizes = [4] * 8
+            gs = [[4]] * 8
             if b == 0:
-                sizes = [4] * 8
+                gs = [[4]] * 8
             if b == B - 1:
-                sizes = [4] * 7 + [2, 1, 1]
+                gs = [[4]] * 7 + [[2], [1], [1]]
             u0 = 0
-            for n in sizes:
-                units.append((b, u0, n))
-                u0 += n
+            for sizes in gs:
+                groups.append((b, u0, sizes))
+                u0 += sum(sizes)
             assert u0 == U
 
         planes = {}
@@ -194,60 +195,74 @@ def tile_jointnetwork_t_kernel(
         o_ps = {}
         o_sbs = {}
         e_pss = {}
-        bank_no = [0]
+        count = {"bank": 0, "planes": 0}
 
-        def new_planes(i):
-            planes[i] = work.tile([P, NCH, UMAX * T], BF16, tag="planes%d" % (i % 4), name="planes_%d" % i)
+        def new_planes(g, k):
+            planes[(g, k)] = work.tile(
+                [P, NCH, UB * T], BF16, tag="planes%d" % (count["planes"] % 4), name="planes_%d_%d" % (g, k)
+            )
+            count["planes"] += 1
 
-        def tanh(i, c, ul):
-            b, u0, n = units[i]
-            col = b * U + u0 + ul
+        def tanh(g, k, c, ul):
+            b, u0, sizes = groups[g]
+            col = b * U + u0 + sum(sizes[:k]) + ul
             nc.scalar.activation(
-                out=planes[i][:, c, ul * T : (ul + 1) * T],
+                out=planes[(g, k)][:, c, ul * T : (ul + 1) * T],
                 in_=enc_t[:, b, c, :],
                 func=ACTF.Tanh,
                 bias=pred_b[:, c, col : col + 1],
                 scale=1.0,
             )
 
-        def r_j(i):
-            n = units[i][2]
-            j_g[i] = work.tile([P, UMAX * T, 4], BF16, tag="j_g%d" % (i % 3), align_bytes=64, name="j_g_%d" % i)
-            regroup(nc.vector.tensor_copy, j_g[i][:, 0 : n * T, :], planes[i][:, :, 0 : n * T])
-
-        def q_j(i):
-            n = units[i][2]
-            j_codes[i] = work.tile([P, UMAX * T], U32, tag="j_codes%d" % (i % 3), align_bytes=64, name="j_codes_%d" % i)
-            j_scales[i] = work.tile([P, UMAX * T], U8, tag="j_scales%d" % (i % 3), align_bytes=64, name="j_scales_%d" % i)
-            quantise(
-                j_codes[i][:, 0 : n * T],
-                j_scales[i][:, 0 : n * T],
-                j_g[i][:, 0 : n * T, :].rearrange("p w j -> p (w j)"),
+        def r_j(g, k):
+            sizes = groups[g][2]
+            if k == 0:
+                j_g[g] = work.tile([P, UMAX * T, 4], BF16, tag="j_g%d" % (g % 3), align_bytes=64, name="j_g_%d" % g)
+            r0 = sum(sizes[:k]) * T
+            n = sizes[k]
+            regroup(
+                nc.scalar.copy if (g, k) in ACT_R else nc.vector.tensor_copy,
+                j_g[g][:, r0 : r0 + n * T, :],
+                planes[(g, k)][:, :, 0 : n * T],
             )
 
-        def mm_j(i):
-            n = units[i][2]
-            o_ps[i] = []
+        def q_j(g):
+            n = sum(groups[g][2])
+            j_codes[g] = work.tile([P, UMAX * T], U32, tag="j_codes%d" % (g % 3), align_bytes=64, name="j_codes_%d" % g)
+            j_scales[g] = work.tile([P, UMAX * T], U8, tag="j_scales%d" % (g % 3), align_bytes=64, name="j_scales_%d" % g)
+            quantise(
+                j_codes[g][:, 0 : n * T],
+                j_scales[g][:, 0 : n * T],
+                j_g[g][:, 0 : n * T, :].rearrange("p w j -> p (w j)"),
+            )
+
+        def mm_j(g):
+            n = sum(groups[g][2])
+            o_ps[g] = []
             for k0 in range(0, n, UB):
-                bank = psum.tile([P, UB, V], F32, tag="o%d" % (bank_no[0] % 4), bufs=1, name="o_ps_%d_%d" % (i, k0))
-                bank_no[0] += 1
-                o_ps[i].append(bank)
+                bank = psum.tile([P, UB, V], F32, tag="o%d" % (count["bank"] % 4), bufs=1, name="o_ps_%d_%d" % (g, k0))
+                count["bank"] += 1
+                o_ps[g].append(bank)
                 for ul in range(k0, min(n, k0 + UB)):
                     rows = slice(ul * T, (ul + 1) * T)
-                    mx(bank[:, ul - k0, :], j_codes[i][:, rows], j_scales[i][:, rows], wo_codes[:], wo_scales[:])
+                    mx(bank[:, ul - k0, :], j_codes[g][:, rows], j_scales[g][:, rows], wo_codes[:], wo_scales[:])
 
-        def evac(i):
-            n = units[i][2]
-            o_sbs[i] = work.tile([P, UMAX, V], F32, tag="o_sb%d" % (i % 6), name="o_sb_%d" % i)
-            for k, bank in enumerate(o_ps[i]):
+        def evac(g):
+            n = sum(groups[g][2])
+            o_sbs[g] = work.tile([P, UMAX, V], F32, tag="o_sb%d" % (g % 6), name="o_sb_%d" % g)
+            for k, bank in enumerate(o_ps[g]):
                 m = min(UB, n - k * UB)
                 nc.vector.tensor_tensor(
-                    out=o_sbs[i][:, k * UB : k * UB + m, :], in0=bank[:, 0:m, :], in1=bo4[:, 0:m, :], op=ALU.add
+                    out=o_sbs[g][:, k * UB : k * UB + m, :],
+                    in0=bank[:, 0:m, :],
+                    in1=bo[:].unsqueeze(1).to_broadcast([P, m, V]),
+                    op=ALU.add,
                 )
 
-        def clamp_store(i):
-            b, u0, n = units[i]
-            o_sb = o_sbs[i]
+        def clamp_store(g):
+            b, u0, sizes = groups[g]
+            n = sum(sizes)
+            o_sb = o_sbs[g]
             nc.vector.tensor_scalar(
                 out=o_sb[:, 0:n, :], in0=o_sb[:, 0:n, :], scalar1=CLAMP, scalar2=-CLAMP, op0=ALU.min, op1=ALU.max
             )
@@ -261,7 +276,7 @@ def tile_jointnetwork_t_kernel(
             cols = slice(k * T, (k + 1) * T)
             gcols = slice(k * T * 4, (k + 1) * T * 4)
             if step == 0:
-                transpose_rows(x_sb[:, b, :], x_g[:, gcols], nc.vector.tensor_copy)
+                transpose_rows(x_sb[:, b, :], x_g[:, gcols], nc.scalar.copy)
             elif step == 1:
                 quantise(x_codes[:, cols], x_scales[:, cols], x_g[:, gcols])
                 e_ps = psum.tile([P, NCH, T], F32, tag="mm", name="e_ps%d" % b)
@@ -271,37 +286,41 @@ def tile_jointnetwork_t_kernel(
             else:
                 nc.scalar.copy(out=enc_t[:, b, :, :], in_=e_pss[b][:])
 
-        for i in range(FIRST):
-            new_planes(i)
+        for g in range(FIRSTG):
+            for k in range(len(groups[g][2])):
+                new_planes(g, k)
         for c in range(NCH):
             nc.scalar.copy(out=enc_t[:, 0, c, :], in_=e0_ps[c][:])
-            for i in range(FIRST):
-                for ul in range(units[i][2]):
-                    tanh(i, c, ul)
-        for i in range(FIRST):
-            r_j(i)
-        for i in range(FIRST):
-            q_j(i)
-            mm_j(i)
+            for g in range(FIRSTG):
+                for k, n in enumerate(groups[g][2]):
+                    for ul in range(n):
+                        tanh(g, k, c, ul)
+        for g in range(FIRSTG):
+            for k in range(len(groups[g][2])):
+                r_j(g, k)
+        for g in range(FIRSTG):
+            q_j(g)
+            mm_j(g)
         done = 0
-        for i in range(FIRST, len(units)):
-            b, u0, n = units[i]
-            new_planes(i)
-            for ul in range(n):
-                for c in range(NCH):
-                    tanh(i, c, ul)
-            r_j(i)
+        for g in range(FIRSTG, len(groups)):
+            b, u0, sizes = groups[g]
+            for k, n in enumerate(sizes):
+                new_planes(g, k)
+                for ul in range(n):
+                    for c in range(NCH):
+                        tanh(g, k, c, ul)
+                r_j(g, k)
             first_new = done
-            while done < i - LAG:
+            while done < g - LAG:
                 evac(done)
                 done += 1
-            q_j(i)
-            mm_j(i)
+            q_j(g)
+            mm_j(g)
             for k in range(first_new, done):
                 clamp_store(k)
             if b + 1 < B and u0 in SETUP_U:
                 setup_x(b + 1, SETUP_U.index(u0))
-        while done < len(units):
+        while done < len(groups):
             evac(done)
             clamp_store(done)
             done += 1

@@ -15,12 +15,9 @@ P = 128
 B, T, U, D, V = 4, 128, 32, 512, 128
 NCH = 4
 UB = 4
-UMAX = 8
 CLAMP = 15.0
 FLOPS = 2 * (B * T * D * D + B * U * D * D + B * T * U * D * V)
-PIN = False
-FIRSTG = 2
-ACT_R = ((10, 0), (21, 0))
+FIRST = 2
 LAG = 1
 SETUP_U = (8, 12, 16)
 
@@ -37,8 +34,6 @@ def tile_jointnetwork_t_kernel(
 ):
     nc = tc.nc
     with ExitStack() as ctx:
-        if PIN:
-            ctx.enter_context(tc.manual_schedule())
         keep = ctx.enter_context(tc.tile_pool(name="keep", bufs=1))
         work = ctx.enter_context(tc.tile_pool(name="work", bufs=1))
         psum = ctx.enter_context(tc.psum_pool(name="psum", bufs=2))
@@ -65,8 +60,7 @@ def tile_jointnetwork_t_kernel(
         bo = keep.tile([P, V], F32)
         y_sb = keep.tile([P, D], BF16)
         x_sb = keep.tile([P, B, D], BF16)
-        we_raw = [keep.tile([P, 4, D // 2], BF16, name="we_raw%d" % h) for h in range(2)]
-        wp_raw = [keep.tile([P, 4, D // 2], BF16, name="wp_raw%d" % h) for h in range(2)]
+        w_raw = [keep.tile([P, 4, 2 * P], BF16, name="w_raw%d" % c) for c in range(NCH)]
         wo_raw = keep.tile([P, NCH, V], BF16)
         xy_g = keep.tile([P, 2 * P * 4], BF16, align_bytes=64)
         xy_codes = keep.tile([P, 2 * P], U32, align_bytes=64)
@@ -92,10 +86,10 @@ def tile_jointnetwork_t_kernel(
         nc.scalar.activation(out=warm[:], in_=warm[:], func=ACTF.Tanh)
         nc.sync.dma_start(out=y_sb[:], in_=predictor_out.rearrange("b u d -> (b u) d"))
         nc.sync.dma_start(out=x_sb[:, 0, :], in_=encoder_out[0])
-        for h in range(2):
-            cols = slice(h * (D // 2), (h + 1) * (D // 2))
-            nc.sync.dma_start(out=we_raw[h][:], in_=W_enc[:, cols].rearrange("(p j) c -> p j c", j=4))
-            nc.sync.dma_start(out=wp_raw[h][:], in_=W_pred[:, cols].rearrange("(p j) c -> p j c", j=4))
+        for c in range(NCH):
+            cols = slice(c * P, (c + 1) * P)
+            nc.sync.dma_start(out=w_raw[c][:, :, 0:P], in_=W_enc[:, cols].rearrange("(p j) c -> p j c", j=4))
+            nc.sync.dma_start(out=w_raw[c][:, :, P : 2 * P], in_=W_pred[:, cols].rearrange("(p j) c -> p j c", j=4))
         nc.sync.dma_start(out=wo_raw[:], in_=W_out.rearrange("(c p) v -> p c v", p=P))
         nc.sync.dma_start(out=x_sb[:, 1:B, :], in_=encoder_out[1:B].rearrange("b t d -> t b d"))
 
@@ -114,78 +108,20 @@ def tile_jointnetwork_t_kernel(
         nc.vector.tensor_copy(out=bf[:], in_=bz[:])
         bt_ps = psum.tile([P, P], F32, tag="tr")
         nc.tensor.transpose(bt_ps[:], bf[:], ident[:])
-        bo_ps = psum.tile([P, V], F32, tag="tr")
-        nc.tensor.matmul(
-            out=bo_ps[:], lhsT=ident[:, 8:9].to_broadcast([P, P]), rhs=bf[:], start=True, stop=True
-        )
-
-        def r_w(raw, c, side):
-            cc = (c % 2) * P
-            regroup(
-                nc.scalar.copy if side == 0 else nc.vector.tensor_copy,
-                w_g[:, c, side * P : (side + 1) * P, :],
-                raw[c // 2][:, :, cc : cc + P],
-            )
-
-        def q_w(c):
-            quantise(w_codes[:, c, :], w_scales[:, c, :], w_g[:, c, :, :].rearrange("p w j -> p (w j)"))
-
-        e0_ps = [None] * NCH
-        p_ps = [None] * NCH
-
-        def mm_chunk(c):
-            e0_ps[c] = psum.tile([P, T], F32, tag="o%d" % c, bufs=1, name="e0_ps_%d" % c)
-            mx(e0_ps[c][:], w_codes[:, c, 0:P], w_scales[:, c, 0:P], xy_codes[:, P : 2 * P], xy_scales[:, P : 2 * P])
-            p_ps[c] = psum.tile([P, B * U], F32, tag="mm", name="p_ps%d" % c)
-            mx(p_ps[c][:], w_codes[:, c, P : 2 * P], w_scales[:, c, P : 2 * P], xy_codes[:, 0:P], xy_scales[:, 0:P])
-
-        def predb(c):
-            nc.vector.tensor_scalar(
-                out=pred_b[:, c, :],
-                in0=p_ps[c][:],
-                scalar1=b_t[:, c : c + 1],
-                scalar2=b_t[:, NCH + c : NCH + c + 1],
-                op0=ALU.add,
-                op1=ALU.add,
-            )
-
-        r_w(we_raw, 0, 0)
-        r_w(we_raw, 1, 0)
-        quantise(xy_codes[:], xy_scales[:], xy_g[:])
         nc.vector.tensor_copy(out=b_t[:], in_=bt_ps[:, 0:8])
-        r_w(wp_raw, 0, 1)
-        r_w(wp_raw, 1, 1)
-        q_w(0)
-        mm_chunk(0)
-        q_w(1)
-        mm_chunk(1)
-        r_w(we_raw, 2, 0)
-        predb(0)
-        r_w(we_raw, 3, 0)
-        predb(1)
-        r_w(wp_raw, 2, 1)
-        r_w(wp_raw, 3, 1)
-        q_w(2)
-        mm_chunk(2)
-        q_w(3)
-        mm_chunk(3)
-        regroup(nc.vector.tensor_copy, wo_g[:], wo_raw[:])
-        predb(2)
-        predb(3)
-        quantise(wo_codes[:], wo_scales[:], wo_g[:].rearrange("p w j -> p (w j)"))
-        nc.vector.tensor_copy(out=bo[:], in_=bo_ps[:])
+        quantise(xy_codes[:], xy_scales[:], xy_g[:])
 
-        groups = []
+        units = []
         for b in range(B):
-            gs = [[4]] * 8
+            sizes = [4] * 8
             if b == 0:
-                gs = [[4]] * 8
+                sizes = [4] * 8
             if b == B - 1:
-                gs = [[4]] * 7 + [[2], [1], [1]]
+                sizes = [4] * 7 + [2, 1, 1]
             u0 = 0
-            for sizes in gs:
-                groups.append((b, u0, sizes))
-                u0 += sum(sizes)
+            for n in sizes:
+                units.append((b, u0, n))
+                u0 += n
             assert u0 == U
 
         planes = {}
@@ -195,75 +131,90 @@ def tile_jointnetwork_t_kernel(
         o_ps = {}
         o_sbs = {}
         e_pss = {}
-        count = {"bank": 0, "planes": 0}
 
-        def new_planes(g, k):
-            planes[(g, k)] = work.tile(
-                [P, NCH, UB * T], BF16, tag="planes%d" % (count["planes"] % 4), name="planes_%d_%d" % (g, k)
-            )
-            count["planes"] += 1
+        def new_planes(i):
+            planes[i] = work.tile([P, NCH, UB * T], BF16, tag="planes%d" % (i % 4), name="planes_%d" % i)
 
-        def tanh(g, k, c, ul):
-            b, u0, sizes = groups[g]
-            col = b * U + u0 + sum(sizes[:k]) + ul
+        def tanh(i, c, ul):
+            b, u0, n = units[i]
+            col = b * U + u0 + ul
             nc.scalar.activation(
-                out=planes[(g, k)][:, c, ul * T : (ul + 1) * T],
+                out=planes[i][:, c, ul * T : (ul + 1) * T],
                 in_=enc_t[:, b, c, :],
                 func=ACTF.Tanh,
                 bias=pred_b[:, c, col : col + 1],
                 scale=1.0,
             )
 
-        def r_j(g, k):
-            sizes = groups[g][2]
-            if k == 0:
-                j_g[g] = work.tile([P, UMAX * T, 4], BF16, tag="j_g%d" % (g % 3), align_bytes=64, name="j_g_%d" % g)
-            r0 = sum(sizes[:k]) * T
-            n = sizes[k]
-            regroup(
-                nc.scalar.copy if (g, k) in ACT_R else nc.vector.tensor_copy,
-                j_g[g][:, r0 : r0 + n * T, :],
-                planes[(g, k)][:, :, 0 : n * T],
-            )
-
-        def q_j(g):
-            n = sum(groups[g][2])
-            j_codes[g] = work.tile([P, UMAX * T], U32, tag="j_codes%d" % (g % 3), align_bytes=64, name="j_codes_%d" % g)
-            j_scales[g] = work.tile([P, UMAX * T], U8, tag="j_scales%d" % (g % 3), align_bytes=64, name="j_scales_%d" % g)
-            quantise(
-                j_codes[g][:, 0 : n * T],
-                j_scales[g][:, 0 : n * T],
-                j_g[g][:, 0 : n * T, :].rearrange("p w j -> p (w j)"),
-            )
-
-        def mm_j(g):
-            n = sum(groups[g][2])
-            o_ps[g] = []
-            for k0 in range(0, n, UB):
-                bank = psum.tile([P, UB, V], F32, tag="o%d" % (count["bank"] % 4), bufs=1, name="o_ps_%d_%d" % (g, k0))
-                count["bank"] += 1
-                o_ps[g].append(bank)
-                for ul in range(k0, min(n, k0 + UB)):
-                    rows = slice(ul * T, (ul + 1) * T)
-                    mx(bank[:, ul - k0, :], j_codes[g][:, rows], j_scales[g][:, rows], wo_codes[:], wo_scales[:])
-
-        def evac(g):
-            n = sum(groups[g][2])
-            o_sbs[g] = work.tile([P, UMAX, V], F32, tag="o_sb%d" % (g % 6), name="o_sb_%d" % g)
-            for k, bank in enumerate(o_ps[g]):
-                m = min(UB, n - k * UB)
-                nc.vector.tensor_tensor(
-                    out=o_sbs[g][:, k * UB : k * UB + m, :],
-                    in0=bank[:, 0:m, :],
-                    in1=bo[:].unsqueeze(1).to_broadcast([P, m, V]),
-                    op=ALU.add,
-                )
-
-        def clamp_store(g):
-            b, u0, sizes = groups[g]
-            n = sum(sizes)
-            o_sb = o_sbs[g]
+        for i in range(FIRST):
+            new_planes(i)
+        for c in range(NCH):
+            regroup(nc.vector.tensor_copy, w_g[:, c, :, :], w_raw[c][:])
+            quantise(w_codes[:, c, :], w_scales[:, c, :], w_g[:, c, :, :].rearrange("p w j -> p (w j)"))
+            p_ps = psum.tile([P, B * U], F32, tag="mm", name="p_ps%d" % c)
+            mx(p_ps[:], w_codes[:, c, P : 2 * P], w_scales[:, c, P : 2 * P], xy_codes[:, 0:P], xy_scales[:, 0:P])
+            e0_ps = psum.tile([P, T], F32, tag="o%d" % c, bufs=1, name="e0_ps_%d" % c)
+            mx(e0_ps[:], w_codes[:, c, 0:P], w_scales[:, c, 0:P], xy_codes[:, P : 2 * P], xy_scales[:, P : 2 * P])
             nc.vector.tensor_scalar(
+                out=pred_b[:, c, :],
+                in0=p_ps[:],
+                scalar1=b_t[:, c : c + 1],
+                scalar2=b_t[:, NCH + c : NCH + c + 1],
+                op0=ALU.add,
+                op1=ALU.add,
+            )
+            if c == 0:
+                nc.scalar.copy(out=enc_t[:, 0, c, :], in_=e0_ps[:])
+            else:
+                nc.vector.tensor_copy(out=enc_t[:, 0, c, :], in_=e0_ps[:])
+            for i in range(FIRST):
+                for ul in range(units[i][2]):
+                    tanh(i, c, ul)
+
+        regroup(nc.vector.tensor_copy, wo_g[:], wo_raw[:])
+        bo_ps = psum.tile([P, V], F32, tag="tr")
+        nc.tensor.matmul(
+            out=bo_ps[:], lhsT=ident[:, 8:9].to_broadcast([P, P]), rhs=bf[:], start=True, stop=True
+        )
+        nc.vector.tensor_copy(out=bo[:], in_=bo_ps[:])
+        quantise(wo_codes[:], wo_scales[:], wo_g[:].rearrange("p w j -> p (w j)"))
+
+        def r_j(i):
+            n = units[i][2]
+            j_g[i] = work.tile([P, UB * T, 4], BF16, tag="j_g%d" % (i % 3), align_bytes=64, name="j_g_%d" % i)
+            regroup(nc.vector.tensor_copy, j_g[i][:, 0 : n * T, :], planes[i][:, :, 0 : n * T])
+
+        def q_j(i):
+            n = units[i][2]
+            j_codes[i] = work.tile([P, UB * T], U32, tag="j_codes%d" % (i % 3), align_bytes=64, name="j_codes_%d" % i)
+            j_scales[i] = work.tile([P, UB * T], U8, tag="j_scales%d" % (i % 3), align_bytes=64, name="j_scales_%d" % i)
+            quantise(
+                j_codes[i][:, 0 : n * T],
+                j_scales[i][:, 0 : n * T],
+                j_g[i][:, 0 : n * T, :].rearrange("p w j -> p (w j)"),
+            )
+
+        def mm_j(i):
+            n = units[i][2]
+            o_ps[i] = psum.tile([P, UB, V], F32, tag="o%d" % (i % 4), bufs=1, name="o_ps_%d" % i)
+            for ul in range(n):
+                rows = slice(ul * T, (ul + 1) * T)
+                mx(o_ps[i][:, ul, :], j_codes[i][:, rows], j_scales[i][:, rows], wo_codes[:], wo_scales[:])
+
+        def evac(i):
+            n = units[i][2]
+            o_sbs[i] = work.tile([P, UB, V], F32, tag="o_sb%d" % (i % 6), name="o_sb_%d" % i)
+            nc.vector.tensor_tensor(
+                out=o_sbs[i][:, 0:n, :],
+                in0=o_ps[i][:, 0:n, :],
+                in1=bo[:].unsqueeze(1).to_broadcast([P, n, V]),
+                op=ALU.add,
+            )
+
+        def clamp_store(i):
+            b, u0, n = units[i]
+            o_sb = o_sbs[i]
+            nc.gpsimd.tensor_scalar(
                 out=o_sb[:, 0:n, :], in0=o_sb[:, 0:n, :], scalar1=CLAMP, scalar2=-CLAMP, op0=ALU.min, op1=ALU.max
             )
             nc.sync.dma_start(
@@ -276,7 +227,7 @@ def tile_jointnetwork_t_kernel(
             cols = slice(k * T, (k + 1) * T)
             gcols = slice(k * T * 4, (k + 1) * T * 4)
             if step == 0:
-                transpose_rows(x_sb[:, b, :], x_g[:, gcols], nc.scalar.copy)
+                transpose_rows(x_sb[:, b, :], x_g[:, gcols], nc.vector.tensor_copy)
             elif step == 1:
                 quantise(x_codes[:, cols], x_scales[:, cols], x_g[:, gcols])
                 e_ps = psum.tile([P, NCH, T], F32, tag="mm", name="e_ps%d" % b)
@@ -284,43 +235,32 @@ def tile_jointnetwork_t_kernel(
                     mx(e_ps[:, c, :], w_codes[:, c, 0:P], w_scales[:, c, 0:P], x_codes[:, cols], x_scales[:, cols])
                 e_pss[b] = e_ps
             else:
-                nc.scalar.copy(out=enc_t[:, b, :, :], in_=e_pss[b][:])
+                nc.vector.tensor_copy(out=enc_t[:, b, :, :], in_=e_pss[b][:])
 
-        for g in range(FIRSTG):
-            for k in range(len(groups[g][2])):
-                new_planes(g, k)
-        for c in range(NCH):
-            nc.scalar.copy(out=enc_t[:, 0, c, :], in_=e0_ps[c][:])
-            for g in range(FIRSTG):
-                for k, n in enumerate(groups[g][2]):
-                    for ul in range(n):
-                        tanh(g, k, c, ul)
-        for g in range(FIRSTG):
-            for k in range(len(groups[g][2])):
-                r_j(g, k)
-        for g in range(FIRSTG):
-            q_j(g)
-            mm_j(g)
+        for i in range(FIRST):
+            r_j(i)
+        for i in range(FIRST):
+            q_j(i)
+            mm_j(i)
         done = 0
-        for g in range(FIRSTG, len(groups)):
-            b, u0, sizes = groups[g]
-            for k, n in enumerate(sizes):
-                new_planes(g, k)
-                for ul in range(n):
-                    for c in range(NCH):
-                        tanh(g, k, c, ul)
-                r_j(g, k)
+        for i in range(FIRST, len(units)):
+            b, u0, n = units[i]
+            new_planes(i)
+            for ul in range(n):
+                for c in range(NCH):
+                    tanh(i, c, ul)
+            r_j(i)
             first_new = done
-            while done < g - LAG:
+            while done < i - LAG:
                 evac(done)
                 done += 1
-            q_j(g)
-            mm_j(g)
+            q_j(i)
+            mm_j(i)
             for k in range(first_new, done):
                 clamp_store(k)
             if b + 1 < B and u0 in SETUP_U:
                 setup_x(b + 1, SETUP_U.index(u0))
-        while done < len(groups):
+        while done < len(units):
             evac(done)
             clamp_store(done)
             done += 1

@@ -19,7 +19,7 @@ CLAMP = 15.0
 FLOPS = 2 * (B * T * D * D + B * U * D * D + B * T * U * D * V)
 FIRST = 2
 LAG = 1
-SETUP_U = (8, 12, 16)
+SETUP_U = (8, 12)
 
 
 def regroup(copy_fn, dst, src):
@@ -74,7 +74,6 @@ def tile_jointnetwork_t_kernel(
         wo_g = keep.tile([P, V, 4], BF16, align_bytes=64)
         wo_codes = keep.tile([P, V], U32, align_bytes=64)
         wo_scales = keep.tile([P, V], U8, align_bytes=64)
-        enc_t = keep.tile([P, B, NCH, T], F32)
         pred_b = keep.tile([P, NCH, B * U], F32)
 
         nc.vector.memset(warm[:], 0.0)
@@ -131,16 +130,23 @@ def tile_jointnetwork_t_kernel(
         o_ps = {}
         o_sbs = {}
         e_pss = {}
+        e0_pss = {}
 
         def new_planes(i):
             planes[i] = work.tile([P, NCH, UB * T], BF16, tag="planes%d" % (i % 4), name="planes_%d" % i)
+
+        def enc_of(i, c):
+            b = units[i][0]
+            if i < FIRST:
+                return e0_pss[c][:]
+            return e_pss[b][:, c, :]
 
         def tanh(i, c, ul):
             b, u0, n = units[i]
             col = b * U + u0 + ul
             nc.scalar.activation(
                 out=planes[i][:, c, ul * T : (ul + 1) * T],
-                in_=enc_t[:, b, c, :],
+                in_=enc_of(i, c),
                 func=ACTF.Tanh,
                 bias=pred_b[:, c, col : col + 1],
                 scale=1.0,
@@ -153,8 +159,8 @@ def tile_jointnetwork_t_kernel(
             quantise(w_codes[:, c, :], w_scales[:, c, :], w_g[:, c, :, :].rearrange("p w j -> p (w j)"))
             p_ps = psum.tile([P, B * U], F32, tag="mm", name="p_ps%d" % c)
             mx(p_ps[:], w_codes[:, c, P : 2 * P], w_scales[:, c, P : 2 * P], xy_codes[:, 0:P], xy_scales[:, 0:P])
-            e0_ps = psum.tile([P, T], F32, tag="o%d" % c, bufs=1, name="e0_ps_%d" % c)
-            mx(e0_ps[:], w_codes[:, c, 0:P], w_scales[:, c, 0:P], xy_codes[:, P : 2 * P], xy_scales[:, P : 2 * P])
+            e0_pss[c] = psum.tile([P, T], F32, tag="o%d" % c, bufs=1, name="e0_ps_%d" % c)
+            mx(e0_pss[c][:], w_codes[:, c, 0:P], w_scales[:, c, 0:P], xy_codes[:, P : 2 * P], xy_scales[:, P : 2 * P])
             nc.vector.tensor_scalar(
                 out=pred_b[:, c, :],
                 in0=p_ps[:],
@@ -163,14 +169,16 @@ def tile_jointnetwork_t_kernel(
                 op0=ALU.add,
                 op1=ALU.add,
             )
-            if c == 0:
-                nc.scalar.copy(out=enc_t[:, 0, c, :], in_=e0_ps[:])
-            else:
-                nc.vector.tensor_copy(out=enc_t[:, 0, c, :], in_=e0_ps[:])
             for i in range(FIRST):
                 for ul in range(units[i][2]):
                     tanh(i, c, ul)
 
+        def enc_mx(b, x_c, x_s):
+            e_pss[b] = psum.tile([P, NCH, T], F32, tag="mm", name="e_ps%d" % b)
+            for c in range(NCH):
+                mx(e_pss[b][:, c, :], w_codes[:, c, 0:P], w_scales[:, c, 0:P], x_c, x_s)
+
+        enc_mx(0, xy_codes[:, P : 2 * P], xy_scales[:, P : 2 * P])
         regroup(nc.vector.tensor_copy, wo_g[:], wo_raw[:])
         bo_ps = psum.tile([P, V], F32, tag="tr")
         nc.tensor.matmul(
@@ -228,14 +236,9 @@ def tile_jointnetwork_t_kernel(
             gcols = slice(k * T * 4, (k + 1) * T * 4)
             if step == 0:
                 transpose_rows(x_sb[:, b, :], x_g[:, gcols], nc.vector.tensor_copy)
-            elif step == 1:
-                quantise(x_codes[:, cols], x_scales[:, cols], x_g[:, gcols])
-                e_ps = psum.tile([P, NCH, T], F32, tag="mm", name="e_ps%d" % b)
-                for c in range(NCH):
-                    mx(e_ps[:, c, :], w_codes[:, c, 0:P], w_scales[:, c, 0:P], x_codes[:, cols], x_scales[:, cols])
-                e_pss[b] = e_ps
             else:
-                nc.vector.tensor_copy(out=enc_t[:, b, :, :], in_=e_pss[b][:])
+                quantise(x_codes[:, cols], x_scales[:, cols], x_g[:, gcols])
+                enc_mx(b, x_codes[:, cols], x_scales[:, cols])
 
         for i in range(FIRST):
             r_j(i)

@@ -24,8 +24,8 @@ SETUP_U = (8, 12)
 
 def regroup(copy_fn, dst, src):
     copy_fn(
-        out=dst.rearrange("p (c i) j -> p c j i", i=4),
-        in_=src.rearrange("p j (c i) -> p c j i", i=4),
+        out=dst.rearrange("p (c i) j -> p c j i", i=8),
+        in_=src.rearrange("p j (c i) -> p c j i", i=8),
     )
 
 

@@ -19,7 +19,7 @@ CLAMP = 15.0
 FLOPS = 2 * (B * T * D * D + B * U * D * D + B * T * U * D * V)
 FIRST = 2
 LAG = 1
-SETUP_U = (8, 12)
+SETUP_U = 12
 
 
 def regroup(copy_fn, dst, src):
@@ -54,6 +54,8 @@ def tile_jointnetwork_t_kernel(
 
         warm = keep.tile([P, 1], F32)
         ident = keep.tile([P, P], F32)
+        ones = keep.tile([P, P], BF16)
+        boz = keep.tile([P, V], BF16)
         bz = keep.tile([P, P], BF16)
         bf = keep.tile([P, P], F32)
         b_t = keep.tile([P, 8], F32)
@@ -76,15 +78,17 @@ def tile_jointnetwork_t_kernel(
         wo_scales = keep.tile([P, V], U8, align_bytes=64)
         pred_b = keep.tile([P, NCH, B * U], F32)
 
-        nc.vector.memset(warm[:], 0.0)
         nc.vector.memset(bz[:], 0.0)
+        nc.vector.memset(warm[:], 0.0)
         make_identity(nc, ident[:])
-        nc.scalar.dma_start(out=bz[0:4, :], in_=b_enc.rearrange("(c p) -> c p", p=P))
-        nc.scalar.dma_start(out=bz[4:8, :], in_=b_pred.rearrange("(c p) -> c p", p=P))
-        nc.scalar.dma_start(out=bz[8:9, :], in_=b_out.rearrange("(o v) -> o v", o=1))
-        nc.scalar.activation(out=warm[:], in_=warm[:], func=ACTF.Tanh)
+        nc.vector.memset(boz[:], 0.0)
+        nc.vector.memset(ones[:], 1.0)
         nc.sync.dma_start(out=y_sb[:], in_=predictor_out.rearrange("b u d -> (b u) d"))
         nc.sync.dma_start(out=x_sb[:, 0, :], in_=encoder_out[0])
+        nc.sync.dma_start(out=bz[0:4, :], in_=b_enc.rearrange("(c p) -> c p", p=P))
+        nc.sync.dma_start(out=bz[4:8, :], in_=b_pred.rearrange("(c p) -> c p", p=P))
+        nc.scalar.dma_start(out=boz[0:1, :], in_=b_out.rearrange("(o v) -> o v", o=1))
+        nc.scalar.activation(out=warm[:], in_=warm[:], func=ACTF.Tanh)
         for c in range(NCH):
             cols = slice(c * P, (c + 1) * P)
             nc.sync.dma_start(out=w_raw[c][:, :, 0:P], in_=W_enc[:, cols].rearrange("(p j) c -> p j c", j=4))
@@ -92,23 +96,25 @@ def tile_jointnetwork_t_kernel(
         nc.sync.dma_start(out=wo_raw[:], in_=W_out.rearrange("(c p) v -> p c v", p=P))
         nc.sync.dma_start(out=x_sb[:, 1:B, :], in_=encoder_out[1:B].rearrange("b t d -> t b d"))
 
-        def transpose_rows(rows_bf16, g_slice, copy_fn):
+        ctx.enter_context(tc.manual_schedule(engines={mybir.EngineType.DVE, mybir.EngineType.Activation, mybir.EngineType.PE}))
+
+        def words_transposed(rows_bf16):
             words = rows_bf16.bitcast(F32).rearrange("r (q h) -> r h q", h=2)
             tr = psum.tile([P, 2, P], F32, tag="tr")
             for h in range(2):
                 nc.tensor.transpose(tr[:, h, :], words[:, h, :], ident[:])
+            return tr
+
+        def words_out(g_slice, tr, copy_fn):
             copy_fn(
                 out=g_slice.bitcast(F32).rearrange("p (r h) -> p r h", h=2),
                 in_=tr[:].rearrange("p h r -> p r h"),
             )
 
-        transpose_rows(y_sb[:], xy_g[:, 0 : P * 4], nc.scalar.copy)
-        transpose_rows(x_sb[:, 0, :], xy_g[:, P * 4 : 2 * P * 4], nc.scalar.copy)
-        nc.vector.tensor_copy(out=bf[:], in_=bz[:])
-        bt_ps = psum.tile([P, P], F32, tag="tr")
-        nc.tensor.transpose(bt_ps[:], bf[:], ident[:])
-        nc.vector.tensor_copy(out=b_t[:], in_=bt_ps[:, 0:8])
-        quantise(xy_codes[:], xy_scales[:], xy_g[:])
+        y_tr = words_transposed(y_sb[:])
+        words_out(xy_g[:, 0 : P * 4], y_tr, nc.scalar.copy)
+        x0_tr = words_transposed(x_sb[:, 0, :])
+        words_out(xy_g[:, P * 4 : 2 * P * 4], x0_tr, nc.scalar.copy)
 
         units = []
         for b in range(B):
@@ -154,16 +160,22 @@ def tile_jointnetwork_t_kernel(
 
         for i in range(FIRST):
             new_planes(i)
-        for c in range(NCH):
-            regroup(nc.vector.tensor_copy, w_g[:, c, :, :], w_raw[c][:])
+        def w_regroup(c):
+            regroup(nc.scalar.copy if c == 1 else nc.vector.tensor_copy, w_g[:, c, :, :], w_raw[c][:])
+
+        p_pss = {}
+
+        def w_mx(c):
             quantise(w_codes[:, c, :], w_scales[:, c, :], w_g[:, c, :, :].rearrange("p w j -> p (w j)"))
-            p_ps = psum.tile([P, B * U], F32, tag="mm", name="p_ps%d" % c)
-            mx(p_ps[:], w_codes[:, c, P : 2 * P], w_scales[:, c, P : 2 * P], xy_codes[:, 0:P], xy_scales[:, 0:P])
+            p_pss[c] = psum.tile([P, B * U], F32, tag="mm", name="p_ps%d" % c)
+            mx(p_pss[c][:], w_codes[:, c, P : 2 * P], w_scales[:, c, P : 2 * P], xy_codes[:, 0:P], xy_scales[:, 0:P])
             e0_pss[c] = psum.tile([P, T], F32, tag="o%d" % c, bufs=1, name="e0_ps_%d" % c)
             mx(e0_pss[c][:], w_codes[:, c, 0:P], w_scales[:, c, 0:P], xy_codes[:, P : 2 * P], xy_scales[:, P : 2 * P])
+
+        def pred(c):
             nc.vector.tensor_scalar(
                 out=pred_b[:, c, :],
-                in0=p_ps[:],
+                in0=p_pss[c][:],
                 scalar1=b_t[:, c : c + 1],
                 scalar2=b_t[:, NCH + c : NCH + c + 1],
                 op0=ALU.add,
@@ -178,14 +190,40 @@ def tile_jointnetwork_t_kernel(
             for c in range(NCH):
                 mx(e_pss[b][:, c, :], w_codes[:, c, 0:P], w_scales[:, c, 0:P], x_c, x_s)
 
-        enc_mx(0, xy_codes[:, P : 2 * P], xy_scales[:, P : 2 * P])
+        w_regroup(0)
+        w_regroup(1)
+        quantise(xy_codes[:], xy_scales[:], xy_g[:])
+        nc.vector.tensor_copy(out=bf[:], in_=bz[:])
+        bt_ps = psum.tile([P, P], F32, tag="tr")
+        nc.tensor.transpose(bt_ps[:], bf[:], ident[:])
+        w_mx(0)
+        nc.vector.tensor_copy(out=b_t[:], in_=bt_ps[:, 0:8])
+        w_mx(1)
+        pred(0)
+        w_regroup(2)
+        pred(1)
+        w_mx(2)
+        w_regroup(3)
+        pred(2)
+        w_mx(3)
         regroup(nc.vector.tensor_copy, wo_g[:], wo_raw[:])
+        pred(3)
         bo_ps = psum.tile([P, V], F32, tag="tr")
-        nc.tensor.matmul(
-            out=bo_ps[:], lhsT=ident[:, 8:9].to_broadcast([P, P]), rhs=bf[:], start=True, stop=True
-        )
-        nc.vector.tensor_copy(out=bo[:], in_=bo_ps[:])
+        nc.tensor.matmul(out=bo_ps[:], lhsT=ones[:], rhs=boz[:], start=True, stop=True)
+        enc_mx(0, xy_codes[:, P : 2 * P], xy_scales[:, P : 2 * P])
         quantise(wo_codes[:], wo_scales[:], wo_g[:].rearrange("p w j -> p (w j)"))
+        nc.vector.tensor_copy(out=bo[:], in_=bo_ps[:])
+        xt_ps = {}
+
+        def x_transpose(k):
+            xt_ps[k] = words_transposed(x_sb[:, k + 1, :])
+
+        def x_copy(k):
+            words_out(x_g[:, k * T * 4 : (k + 1) * T * 4], xt_ps[k], nc.vector.tensor_copy)
+
+        def x_quantise(k):
+            cols = slice(k * T, (k + 1) * T)
+            quantise(x_codes[:, cols], x_scales[:, cols], x_g[:, k * T * 4 : (k + 1) * T * 4])
 
         def r_j(i):
             n = units[i][2]
@@ -230,21 +268,13 @@ def tile_jointnetwork_t_kernel(
                 in_=o_sb[:, 0:n, :].rearrange("p u v -> p (u v)"),
             )
 
-        def setup_x(b, step):
-            k = b - 1
-            cols = slice(k * T, (k + 1) * T)
-            gcols = slice(k * T * 4, (k + 1) * T * 4)
-            if step == 0:
-                transpose_rows(x_sb[:, b, :], x_g[:, gcols], nc.vector.tensor_copy)
-            else:
-                quantise(x_codes[:, cols], x_scales[:, cols], x_g[:, gcols])
-                enc_mx(b, x_codes[:, cols], x_scales[:, cols])
-
         for i in range(FIRST):
             r_j(i)
         for i in range(FIRST):
             q_j(i)
             mm_j(i)
+        x_transpose(0)
+        x_transpose(1)
         done = 0
         for i in range(FIRST, len(units)):
             b, u0, n = units[i]
@@ -261,8 +291,16 @@ def tile_jointnetwork_t_kernel(
             mm_j(i)
             for k in range(first_new, done):
                 clamp_store(k)
-            if b + 1 < B and u0 in SETUP_U:
-                setup_x(b + 1, SETUP_U.index(u0))
+            step = i - FIRST
+            if 1 <= step <= B - 1:
+                x_quantise(step - 1)
+            if step < B - 1:
+                x_copy(step)
+                if step == 0:
+                    x_transpose(2)
+            if b + 1 < B and u0 == SETUP_U:
+                cols = slice(b * T, (b + 1) * T)
+                enc_mx(b + 1, x_codes[:, cols], x_scales[:, cols])
         while done < len(units):
             evac(done)
             clamp_store(done)

@@ -161,7 +161,11 @@ def tile_jointnetwork_t_kernel(
         for i in range(FIRST):
             new_planes(i)
         def w_regroup(c):
-            regroup(nc.scalar.copy if c == 1 else nc.vector.tensor_copy, w_g[:, c, :, :], w_raw[c][:])
+            if c == 0:
+                regroup(nc.scalar.copy, w_g[:, c, P : 2 * P, :], w_raw[c][:, :, P : 2 * P])
+                regroup(nc.vector.tensor_copy, w_g[:, c, 0:P, :], w_raw[c][:, :, 0:P])
+            else:
+                regroup(nc.vector.tensor_copy, w_g[:, c, :, :], w_raw[c][:])
 
         p_pss = {}
 
@@ -190,16 +194,16 @@ def tile_jointnetwork_t_kernel(
             for c in range(NCH):
                 mx(e_pss[b][:, c, :], w_codes[:, c, 0:P], w_scales[:, c, 0:P], x_c, x_s)
 
-        w_regroup(0)
-        w_regroup(1)
-        quantise(xy_codes[:], xy_scales[:], xy_g[:])
         nc.vector.tensor_copy(out=bf[:], in_=bz[:])
         bt_ps = psum.tile([P, P], F32, tag="tr")
         nc.tensor.transpose(bt_ps[:], bf[:], ident[:])
-        w_mx(0)
+        w_regroup(0)
         nc.vector.tensor_copy(out=b_t[:], in_=bt_ps[:, 0:8])
-        w_mx(1)
+        quantise(xy_codes[:], xy_scales[:], xy_g[:])
+        w_mx(0)
+        w_regroup(1)
         pred(0)
+        w_mx(1)
         w_regroup(2)
         pred(1)
         w_mx(2)
@@ -257,12 +261,16 @@ def tile_jointnetwork_t_kernel(
                 op=ALU.add,
             )
 
+        def clamp(engine, cols):
+            engine.tensor_scalar(out=cols, in0=cols, scalar1=CLAMP, scalar2=-CLAMP, op0=ALU.min, op1=ALU.max)
+
         def clamp_store(i):
             b, u0, n = units[i]
             o_sb = o_sbs[i]
-            nc.gpsimd.tensor_scalar(
-                out=o_sb[:, 0:n, :], in0=o_sb[:, 0:n, :], scalar1=CLAMP, scalar2=-CLAMP, op0=ALU.min, op1=ALU.max
-            )
+            cols = o_sb[:].rearrange("p u v -> p (u v)")
+            clamp(nc.vector, cols[:, 0:V])
+            if n > 1:
+                clamp(nc.gpsimd, cols[:, V - 1 : n * V])
             nc.sync.dma_start(
                 out=out[b].rearrange("t u v -> t (u v)")[:, u0 * V : (u0 + n) * V],
                 in_=o_sb[:, 0:n, :].rearrange("p u v -> p (u v)"),

@@ -137,6 +137,7 @@ def tile_jointnetwork_t_kernel(
         o_sbs = {}
         e_pss = {}
         e0_pss = {}
+        enc_t = {}
 
         def new_planes(i):
             planes[i] = work.tile([P, NCH, UB * T], BF16, tag="planes%d" % (i % 4), name="planes_%d" % i)
@@ -145,7 +146,7 @@ def tile_jointnetwork_t_kernel(
             b = units[i][0]
             if i < FIRST:
                 return e0_pss[c][:]
-            return e_pss[b][:, c, :]
+            return enc_t[b][:, c, :]
 
         def tanh(i, c, ul):
             b, u0, n = units[i]
@@ -216,6 +217,12 @@ def tile_jointnetwork_t_kernel(
         nc.tensor.matmul(out=bo_ps[:], lhsT=ones[:], rhs=boz[:], start=True, stop=True)
         enc_mx(0, xy_codes[:, P : 2 * P], xy_scales[:, P : 2 * P])
         quantise(wo_codes[:], wo_scales[:], wo_g[:].rearrange("p w j -> p (w j)"))
+
+        def enc_out(b):
+            enc_t[b] = keep.tile([P, NCH, T], F32, name="enc_t%d" % b)
+            nc.vector.tensor_copy(out=enc_t[b][:], in_=e_pss[b][:])
+
+        enc_out(0)
         nc.vector.tensor_copy(out=bo[:], in_=bo_ps[:])
         xt_ps = {}
 
@@ -309,6 +316,8 @@ def tile_jointnetwork_t_kernel(
             if b + 1 < B and u0 == SETUP_U:
                 cols = slice(b * T, (b + 1) * T)
                 enc_mx(b + 1, x_codes[:, cols], x_scales[:, cols])
+            if b + 1 < B and u0 == SETUP_U + UB:
+                enc_out(b + 1)
         while done < len(units):
             evac(done)
             clamp_store(done)

from contextlib import ExitStack

import concourse.mybir as mybir
from concourse.masks import make_identity

F32 = mybir.dt.float32
BF16 = mybir.dt.bfloat16
U32 = mybir.dt.uint32
U8 = mybir.dt.uint8
FP8X4 = mybir.dt.float8_e4m3fn_x4
ACTF = mybir.ActivationFunctionType
ALU = mybir.AluOpType

P = 128
B, T, U, D, V = 4, 128, 32, 512, 128
NCH = 4
UB = 4
CLAMP = 15.0
FLOPS = 2 * (B * T * D * D + B * U * D * D + B * T * U * D * V)
FIRST = 2
LAG = 1
SETUP_U = 12


def regroup(copy_fn, dst, src):
    copy_fn(
        out=dst.rearrange("p (c i) j -> p c j i", i=8),
        in_=src.rearrange("p j (c i) -> p c j i", i=8),
    )


def tile_jointnetwork_t_kernel(
    tc, encoder_out, predictor_out, W_enc, b_enc, W_pred, b_pred, W_out, b_out, out
):
    nc = tc.nc
    with ExitStack() as ctx:
        keep = ctx.enter_context(tc.tile_pool(name="keep", bufs=1))
        work = ctx.enter_context(tc.tile_pool(name="work", bufs=1))
        psum = ctx.enter_context(tc.psum_pool(name="psum", bufs=2))

        def quantise(codes, scales, grouped):
            nc.vector.quantize_mx(out=codes.bitcast(FP8X4), scales=scales, in_=grouped)

        def mx(out_ps, l_codes, l_scales, r_codes, r_scales):
            nc.tensor.matmul_mx(
                out=out_ps,
                lhsT=l_codes.bitcast(FP8X4),
                lhsT_scale=l_scales,
                rhs=r_codes.bitcast(FP8X4),
                rhs_scale=r_scales,
                start=True,
                stop=True,
            )

        warm = keep.tile([P, 1], F32)
        ident = keep.tile([P, P], F32)
        ones = keep.tile([P, P], BF16)
        boz = keep.tile([P, V], BF16)
        bz = keep.tile([P, P], BF16)
        bf = keep.tile([P, P], F32)
        b_t = keep.tile([P, 8], F32)
        bo = keep.tile([P, V], F32)
        y_sb = keep.tile([P, D], BF16)
        x_sb = keep.tile([P, B, D], BF16)
        w_raw = [keep.tile([P, 4, 2 * P], BF16, name="w_raw%d" % c) for c in range(NCH)]
        wo_raw = keep.tile([P, NCH, V], BF16)
        xy_g = keep.tile([P, 2 * P * 4], BF16, align_bytes=64)
        xy_codes = keep.tile([P, 2 * P], U32, align_bytes=64)
        xy_scales = keep.tile([P, 2 * P], U8, align_bytes=64)
        x_g = keep.tile([P, (B - 1) * T * 4], BF16, align_bytes=64)
        x_codes = keep.tile([P, (B - 1) * T], U32, align_bytes=64)
        x_scales = keep.tile([P, (B - 1) * T], U8, align_bytes=64)
        w_g = keep.tile([P, NCH, 2 * P, 4], BF16, align_bytes=64)
        w_codes = keep.tile([P, NCH, 2 * P], U32, align_bytes=64)
        w_scales = keep.tile([P, NCH, 2 * P], U8, align_bytes=64)
        wo_g = keep.tile([P, V, 4], BF16, align_bytes=64)
        wo_codes = keep.tile([P, V], U32, align_bytes=64)
        wo_scales = keep.tile([P, V], U8, align_bytes=64)
        pred_b = keep.tile([P, NCH, B * U], F32)

        nc.vector.memset(bz[:], 0.0)
        nc.vector.memset(warm[:], 0.0)
        make_identity(nc, ident[:])
        nc.vector.memset(boz[:], 0.0)
        nc.vector.memset(ones[:], 1.0)
        nc.sync.dma_start(out=y_sb[:], in_=predictor_out.rearrange("b u d -> (b u) d"))
        nc.sync.dma_start(out=x_sb[:, 0, :], in_=encoder_out[0])
        nc.sync.dma_start(out=bz[0:4, :], in_=b_enc.rearrange("(c p) -> c p", p=P))
        nc.sync.dma_start(out=bz[4:8, :], in_=b_pred.rearrange("(c p) -> c p", p=P))
        nc.scalar.dma_start(out=boz[0:1, :], in_=b_out.rearrange("(o v) -> o v", o=1))
        nc.scalar.activation(out=warm[:], in_=warm[:], func=ACTF.Tanh)
        for c in range(NCH):
            cols = slice(c * P, (c + 1) * P)
            nc.sync.dma_start(out=w_raw[c][:, :, 0:P], in_=W_enc[:, cols].rearrange("(p j) c -> p j c", j=4))
            nc.sync.dma_start(out=w_raw[c][:, :, P : 2 * P], in_=W_pred[:, cols].rearrange("(p j) c -> p j c", j=4))
        nc.sync.dma_start(out=wo_raw[:], in_=W_out.rearrange("(c p) v -> p c v", p=P))
        nc.sync.dma_start(out=x_sb[:, 1:B, :], in_=encoder_out[1:B].rearrange("b t d -> t b d"))

        ctx.enter_context(tc.manual_schedule(engines={mybir.EngineType.DVE, mybir.EngineType.Activation, mybir.EngineType.PE}))

        def words_transposed(rows_bf16):
            words = rows_bf16.bitcast(F32).rearrange("r (q h) -> r h q", h=2)
            tr = psum.tile([P, 2, P], F32, tag="tr")
            for h in range(2):
                nc.tensor.transpose(tr[:, h, :], words[:, h, :], ident[:])
            return tr

        def words_out(g_slice, tr, copy_fn):
            copy_fn(
                out=g_slice.bitcast(F32).rearrange("p (r h) -> p r h", h=2),
                in_=tr[:].rearrange("p h r -> p r h"),
            )

        y_tr = words_transposed(y_sb[:])
        words_out(xy_g[:, 0 : P * 4], y_tr, nc.scalar.copy)
        x0_tr = words_transposed(x_sb[:, 0, :])
        words_out(xy_g[:, P * 4 : 2 * P * 4], x0_tr, nc.scalar.copy)

        units = []
        for b in range(B):
            sizes = [4] * 8
            if b == 0:
                sizes = [4] * 8
            if b == B - 1:
                sizes = [4] * 7 + [2, 1, 1]
            u0 = 0
            for n in sizes:
                units.append((b, u0, n))
                u0 += n
            assert u0 == U

        planes = {}
        j_codes = {}
        j_scales = {}
        j_g = {}
        o_ps = {}
        o_sbs = {}
        e_pss = {}
        e0_pss = {}
        enc_t = {}

        def new_planes(i):
            planes[i] = work.tile([P, NCH, UB * T], BF16, tag="planes%d" % (i % 4), name="planes_%d" % i)

        def enc_of(i, c):
            b = units[i][0]
            if i < FIRST:
                return e0_pss[c][:]
            return enc_t[b][:, c, :]

        def tanh(i, c, ul):
            b, u0, n = units[i]
            col = b * U + u0 + ul
            nc.scalar.activation(
                out=planes[i][:, c, ul * T : (ul + 1) * T],
                in_=enc_of(i, c),
                func=ACTF.Tanh,
                bias=pred_b[:, c, col : col + 1],
                scale=1.0,
            )

        for i in range(FIRST):
            new_planes(i)
        def w_regroup(c):
            if c == 0:
                regroup(nc.scalar.copy, w_g[:, c, P : 2 * P, :], w_raw[c][:, :, P : 2 * P])
                regroup(nc.vector.tensor_copy, w_g[:, c, 0:P, :], w_raw[c][:, :, 0:P])
            else:
                regroup(nc.vector.tensor_copy, w_g[:, c, :, :], w_raw[c][:])

        p_pss = {}

        def w_mx(c):
            quantise(w_codes[:, c, :], w_scales[:, c, :], w_g[:, c, :, :].rearrange("p w j -> p (w j)"))
            p_pss[c] = psum.tile([P, B * U], F32, tag="mm", name="p_ps%d" % c)
            mx(p_pss[c][:], w_codes[:, c, P : 2 * P], w_scales[:, c, P : 2 * P], xy_codes[:, 0:P], xy_scales[:, 0:P])
            e0_pss[c] = psum.tile([P, T], F32, tag="o%d" % c, bufs=1, name="e0_ps_%d" % c)
            mx(e0_pss[c][:], w_codes[:, c, 0:P], w_scales[:, c, 0:P], xy_codes[:, P : 2 * P], xy_scales[:, P : 2 * P])

        def pred(c):
            nc.vector.tensor_scalar(
                out=pred_b[:, c, :],
                in0=p_pss[c][:],
                scalar1=b_t[:, c : c + 1],
                scalar2=b_t[:, NCH + c : NCH + c + 1],
                op0=ALU.add,
                op1=ALU.add,
            )
            for i in range(FIRST):
                for ul in range(units[i][2]):
                    tanh(i, c, ul)

        def enc_mx(b, x_c, x_s):
            e_pss[b] = psum.tile([P, NCH, T], F32, tag="mm", name="e_ps%d" % b)
            for c in range(NCH):
                mx(e_pss[b][:, c, :], w_codes[:, c, 0:P], w_scales[:, c, 0:P], x_c, x_s)

        nc.vector.tensor_copy(out=bf[:], in_=bz[:])
        bt_ps = psum.tile([P, P], F32, tag="tr")
        nc.tensor.transpose(bt_ps[:], bf[:], ident[:])
        w_regroup(0)
        nc.vector.tensor_copy(out=b_t[:], in_=bt_ps[:, 0:8])
        quantise(xy_codes[:], xy_scales[:], xy_g[:])
        w_mx(0)
        w_regroup(1)
        pred(0)
        w_mx(1)
        w_regroup(2)
        pred(1)
        w_mx(2)
        w_regroup(3)
        pred(2)
        w_mx(3)
        regroup(nc.vector.tensor_copy, wo_g[:], wo_raw[:])
        pred(3)
        bo_ps = psum.tile([P, V], F32, tag="tr")
        nc.tensor.matmul(out=bo_ps[:], lhsT=ones[:], rhs=boz[:], start=True, stop=True)
        enc_mx(0, xy_codes[:, P : 2 * P], xy_scales[:, P : 2 * P])
        quantise(wo_codes[:], wo_scales[:], wo_g[:].rearrange("p w j -> p (w j)"))

        def enc_out(b):
            enc_t[b] = keep.tile([P, NCH, T], F32, name="enc_t%d" % b)
            nc.vector.tensor_copy(out=enc_t[b][:], in_=e_pss[b][:])

        enc_out(0)
        nc.vector.tensor_copy(out=bo[:], in_=bo_ps[:])
        xt_ps = {}

        def x_transpose(k):
            xt_ps[k] = words_transposed(x_sb[:, k + 1, :])

        def x_copy(k):
            words_out(x_g[:, k * T * 4 : (k + 1) * T * 4], xt_ps[k], nc.vector.tensor_copy)

        def x_quantise(k):
            cols = slice(k * T, (k + 1) * T)
            quantise(x_codes[:, cols], x_scales[:, cols], x_g[:, k * T * 4 : (k + 1) * T * 4])

        def r_j(i):
            n = units[i][2]
            j_g[i] = work.tile([P, UB * T, 4], BF16, tag="j_g%d" % (i % 3), align_bytes=64, name="j_g_%d" % i)
            regroup(nc.vector.tensor_copy, j_g[i][:, 0 : n * T, :], planes[i][:, :, 0 : n * T])

        def q_j(i):
            n = units[i][2]
            j_codes[i] = work.tile([P, UB * T], U32, tag="j_codes%d" % (i % 3), align_bytes=64, name="j_codes_%d" % i)
            j_scales[i] = work.tile([P, UB * T], U8, tag="j_scales%d" % (i % 3), align_bytes=64, name="j_scales_%d" % i)
            quantise(
                j_codes[i][:, 0 : n * T],
                j_scales[i][:, 0 : n * T],
                j_g[i][:, 0 : n * T, :].rearrange("p w j -> p (w j)"),
            )

        def mm_j(i):
            n = units[i][2]
            o_ps[i] = psum.tile([P, UB, V], F32, tag="o%d" % (i % 4), bufs=1, name="o_ps_%d" % i)
            for ul in range(n):
                rows = slice(ul * T, (ul + 1) * T)
                mx(o_ps[i][:, ul, :], j_codes[i][:, rows], j_scales[i][:, rows], wo_codes[:], wo_scales[:])

        def evac(i):
            n = units[i][2]
            o_sbs[i] = work.tile([P, UB, V], F32, tag="o_sb%d" % (i % 6), name="o_sb_%d" % i)
            nc.vector.tensor_tensor(
                out=o_sbs[i][:, 0:n, :],
                in0=o_ps[i][:, 0:n, :],
                in1=bo[:].unsqueeze(1).to_broadcast([P, n, V]),
                op=ALU.add,
            )

        def clamp(engine, cols):
            engine.tensor_scalar(out=cols, in0=cols, scalar1=CLAMP, scalar2=-CLAMP, op0=ALU.min, op1=ALU.max)

        def clamp_store(i):
            b, u0, n = units[i]
            o_sb = o_sbs[i]
            cols = o_sb[:].rearrange("p u v -> p (u v)")
            clamp(nc.vector, cols[:, 0:V])
            if n > 1:
                clamp(nc.gpsimd, cols[:, V - 1 : n * V])
            nc.sync.dma_start(
                out=out[b].rearrange("t u v -> t (u v)")[:, u0 * V : (u0 + n) * V],
                in_=o_sb[:, 0:n, :].rearrange("p u v -> p (u v)"),
            )

        for i in range(FIRST):
            r_j(i)
        for i in range(FIRST):
            q_j(i)
            mm_j(i)
        x_transpose(0)
        x_transpose(1)
        done = 0
        for i in range(FIRST, len(units)):
            b, u0, n = units[i]
            new_planes(i)
            for ul in range(n):
                for c in range(NCH):
                    tanh(i, c, ul)
            r_j(i)
            first_new = done
            while done < i - LAG:
                evac(done)
                done += 1
            q_j(i)
            mm_j(i)
            for k in range(first_new, done):
                clamp_store(k)
            step = i - FIRST
            if 1 <= step <= B - 1:
                x_quantise(step - 1)
            if step < B - 1:
                x_copy(step)
                if step == 0:
                    x_transpose(2)
            if b + 1 < B and u0 == SETUP_U:
                cols = slice(b * T, (b + 1) * T)
                enc_mx(b + 1, x_codes[:, cols], x_scales[:, cols])
            if b + 1 < B and u0 == SETUP_U + UB:
                enc_out(b + 1)
        while done < len(units):
            evac(done)
            clamp_store(done)
            done += 1
